import numpy as np
import ml_dtypes


def mxq(x, axis, fmt="e4m3"):
    dtype, down = {"e4m3": (ml_dtypes.float8_e4m3fn, 7), "e5m2": (ml_dtypes.float8_e5m2, 14)}[fmt]
    v = np.moveaxis(np.asarray(x, np.float32).astype(ml_dtypes.bfloat16).astype(np.float64), axis, -1)
    blocks = v.reshape(v.shape[:-1] + (-1, 32))
    amax = np.abs(blocks).max(-1, keepdims=True)
    byte = np.maximum(np.where(amax > 0, np.frexp(amax)[1] - 1 + 127, 0) - down, 1)
    scale = np.exp2(byte - 127.0)
    codes = (blocks / scale).astype(np.float32).astype(dtype).astype(np.float64)
    return np.moveaxis((codes * scale).reshape(v.shape), -1, axis)


WIDE = False


def mx_kscale(k):
    if not WIDE:
        return np.ones(k)
    levels = np.array([10, -10, 5, -5, 0])
    if k % 512:
        return np.exp2(np.random.permutation(np.resize(levels, k // 32))).repeat(32)
    a = np.empty((k // 512, 16))
    for p in range(k // 512):
        a[p, :8] = np.random.permutation(np.resize(levels, 8))
        for g in range(8):
            far = levels[np.abs(levels - a[p, g]) >= 10]
            a[p, g + 8] = far[np.random.randint(len(far))]
    return np.exp2(a.ravel()).repeat(32)


BF16 = ml_dtypes.bfloat16


def bf(x):
    return np.asarray(x, np.float32).astype(BF16)


def f64(x):
    return np.asarray(x).astype(np.float64)


L, B, D, D0 = 512, 8, 512, 768
EPS_BN = 1e-5
EPS_LN = 1e-5


def setup_inputs():
    n = np.random.standard_normal
    s = mx_kscale(D)
    r = n((B, L, D))
    return {"x": bf(n((L, B, D))), "res_a": bf(np.where(r > 0, r, 0.25 * r)),
            "ctx_v": bf(n((B, L, D)) * 0.25 * s), "W_v": bf(n((D, D)) * 2.0 / np.sqrt(D) / s[None, :]),
            "bn_v_g": bf(1.0 + 0.1 * n(D)), "bn_v_b": bf(0.2 * n(D)),
            "prelu_v": bf(0.25 + 0.05 * n(1)), "ln_g": bf(1.0 + 0.1 * n(D)), "ln_b": bf(0.2 * n(D))}


def reference(x, res_a, ctx_v, W_v, bn_v_g, bn_v_b, prelu_v, ln_g, ln_b):
    xq = np.swapaxes(f64(x), 0, 1)
    y = mxq(f64(ctx_v), 2, "e4m3") @ mxq(f64(W_v), 1, "e4m3").T
    mean = y.mean(axis=(0, 1))
    var = y.var(axis=(0, 1))
    z = (y - mean) / np.sqrt(var + EPS_BN) * f64(bn_v_g) + f64(bn_v_b)
    res_v = np.where(z > 0, z, f64(prelu_v) * z)
    out = np.swapaxes(xq + f64(res_a) + res_v, 0, 1)
    mu = out.mean(axis=-1, keepdims=True)
    v = out.var(axis=-1, keepdims=True)
    return (out - mu) / np.sqrt(v + EPS_LN) * f64(ln_g) + f64(ln_b)

@@ -1,0 +1,304 @@
+from contextlib import ExitStack
+
+import concourse.mybir as mybir
+from concourse.masks import make_identity
+
+F32 = mybir.dt.float32
+BF16 = mybir.dt.bfloat16
+U32 = mybir.dt.uint32
+U8 = mybir.dt.uint8
+FP8X4 = mybir.dt.float8_e4m3fn_x4
+ALU = mybir.AluOpType
+ACT = mybir.ActivationFunctionType
+
+L, B, D = 512, 8, 512
+P = 128
+EPS_BN = 1e-5
+EPS_LN = 1e-5
+TILES = 4
+BLOCKS = L * B // (TILES * P)
+CHUNKS = D // P
+WORDS = D // 2
+HELPED = 2
+FLOPS = 2 * L * B * D * D
+
+
+def tile_coattention_pb_t_kernel(tc, x, res_a, ctx_v, W_v, bn_v_g, bn_v_b, prelu_v, ln_g, ln_b, out):
+    nc = tc.nc
+    with ExitStack() as stack:
+        stack.enter_context(tc.manual_schedule())
+        const = stack.enter_context(tc.tile_pool(name="const", bufs=1))
+        keep = stack.enter_context(tc.tile_pool(name="keep", bufs=1))
+        branch = stack.enter_context(tc.tile_pool(name="branch", bufs=2 * CHUNKS))
+        scrap = stack.enter_context(tc.tile_pool(name="scrap", bufs=4))
+        small = stack.enter_context(tc.tile_pool(name="small", bufs=3))
+        gain_psum = stack.enter_context(tc.psum_pool(name="gain_psum", bufs=1))
+        y_psum = stack.enter_context(tc.psum_pool(name="y_psum", bufs=3))
+        turn_psum = stack.enter_context(tc.psum_pool(name="turn_psum", bufs=4))
+
+        def block_rows(blk):
+            group, half = divmod(blk, B // TILES)
+            return slice(group * P, (group + 1) * P), slice(half * TILES, (half + 1) * TILES)
+
+        eps_bn = const.tile([P, 1], F32, name="eps_bn")
+        nc.vector.memset(eps_bn[:], EPS_BN)
+        eps_ln = const.tile([P, 1], F32, name="eps_ln")
+        nc.vector.memset(eps_ln[:], EPS_LN)
+        warm = const.tile([P, 1], F32, name="warm")
+        nc.scalar.activation(out=warm[:], in_=eps_bn[:], func=ACT.Abs_reciprocal_sqrt)
+
+        ones = const.tile([P, P], BF16, name="ones")
+        nc.vector.memset(ones[:], 1.0)
+        bn_rows = const.tile([P, P], BF16, name="bn_rows")
+        nc.vector.memset(bn_rows[:], 0.0)
+        ln_rows = const.tile([P, 2, D], BF16, name="ln_rows")
+        nc.vector.memset(ln_rows[:], 0.0)
+        slope_bf = const.tile([P, 1], BF16, name="slope_bf")
+        nc.scalar.dma_start(out=bn_rows[0:CHUNKS, :], in_=bn_v_g.rearrange("(c p) -> c p", p=P))
+        nc.scalar.dma_start(out=bn_rows[CHUNKS : 2 * CHUNKS, :], in_=bn_v_b.rearrange("(c p) -> c p", p=P))
+        nc.scalar.dma_start(out=ln_rows[0:1, 0, :], in_=ln_g.rearrange("(o d) -> o d", o=1))
+        nc.scalar.dma_start(out=ln_rows[0:1, 1, :], in_=ln_b.rearrange("(o d) -> o d", o=1))
+        nc.scalar.dma_start(out=slope_bf[:], in_=prelu_v.partition_broadcast(P))
+        ident_f32 = const.tile([P, P], F32, name="ident_f32")
+        make_identity(nc, ident_f32[:])
+        ident_bf = const.tile([P, P], BF16, name="ident_bf")
+        make_identity(nc, ident_bf[:])
+
+        with tc.tile_pool(name="ctx", bufs=4) as ctx_pool, tc.tile_pool(name="stage", bufs=3) as stage:
+            w_sb = keep.tile([P, CHUNKS * D], BF16, name="w_sb")
+            nc.sync.dma_start(
+                out=w_sb[:].rearrange("p (c k) -> p c k", c=CHUNKS), in_=W_v.rearrange("(c p) k -> p c k", p=P)
+            )
+            ctx_sb = []
+            for blk in range(BLOCKS):
+                l_rows, b_rows = block_rows(blk)
+                ctx_t = ctx_pool.tile([P, TILES * D], BF16, name="ctx_t")
+                nc.sync.dma_start(
+                    out=ctx_t[:].rearrange("p (b k) -> p b k", b=TILES),
+                    in_=ctx_v[b_rows, l_rows, :].rearrange("b l k -> l b k"),
+                )
+                ctx_sb.append(ctx_t)
+            x_sb, res_sb = [], []
+            for blk in range(BLOCKS):
+                l_rows, b_rows = block_rows(blk)
+                x_t = keep.tile([P, TILES, D], BF16, name="x_t%d" % blk)
+                nc.sync.dma_start(out=x_t[:], in_=x[l_rows, b_rows, :])
+                res_t = keep.tile([P, TILES, D], BF16, name="res_t%d" % blk)
+                nc.sync.dma_start(out=res_t[:], in_=res_a[b_rows, l_rows, :].rearrange("b l d -> l b d"))
+                x_sb.append(x_t)
+                res_sb.append(res_t)
+
+            w_codes = keep.tile([P, D], U32, name="w_codes", align_bytes=64)
+            w_scales = keep.tile([P, D], U8, name="w_scales", align_bytes=64)
+            ctx_codes = keep.tile([P, BLOCKS, TILES * P], U32, name="ctx_codes", align_bytes=64)
+            ctx_scales = keep.tile([P, BLOCKS, TILES * P], U8, name="ctx_scales", align_bytes=64)
+
+            def turn_k_onto_partitions(rows_sb):
+                words = rows_sb[:].bitcast(F32)
+                grouped = stage.tile([P, TILES * P * 4], BF16, name="grouped", align_bytes=64)
+                grouped_words = grouped[:].bitcast(F32).rearrange("p (c u) -> p c u", u=2)
+                for pair in range(TILES // 2):
+                    turned = turn_psum.tile([P, 2, 2 * P], F32, name="turned", tag="turn")
+                    for i in range(2):
+                        for u in range(2):
+                            row_words = (2 * pair + i) * WORDS
+                            nc.tensor.transpose(
+                                out=turned[:, u, i * P : (i + 1) * P], in_=words[:, row_words + u : row_words + WORDS : 2], identity=ident_f32[:]
+                            )
+                    nc.scalar.copy(
+                        out=grouped_words[:, 2 * pair * P : 2 * (pair + 1) * P, :], in_=turned[:].rearrange("p u r -> p r u")
+                    )
+                return grouped
+
+            def conv_pass(blk, chunk, bank_pool, bank_tag):
+                y_t = bank_pool.tile([P, TILES * P], F32, name="y_t", tag=bank_tag)
+                c_cols = slice(chunk * P, (chunk + 1) * P)
+                nc.tensor.matmul_mx(
+                    out=y_t[:],
+                    lhsT=w_codes[:, c_cols].bitcast(FP8X4),
+                    lhsT_scale=w_scales[:, c_cols],
+                    rhs=ctx_codes[:, blk, :].bitcast(FP8X4),
+                    rhs_scale=ctx_scales[:, blk, :],
+                    start=True,
+                    stop=True,
+                )
+                return y_t
+
+            grouped = {}
+            stats = keep.tile([P, CHUNKS, BLOCKS, 6], F32, name="stats")
+
+            def quantise(blk):
+                nc.vector.quantize_mx(
+                    out=ctx_codes[:, blk, :].bitcast(FP8X4), scales=ctx_scales[:, blk, :], in_=grouped[blk][:]
+                )
+
+            def multiply(blk):
+                if blk + 2 < BLOCKS:
+                    grouped[blk + 2] = turn_k_onto_partitions(ctx_sb[blk + 2])
+                if blk + 1 < BLOCKS:
+                    quantise(blk + 1)
+                for chunk in range(CHUNKS):
+                    if chunk % 2 == 0:
+                        y_t = conv_pass(blk, chunk, y_psum, "y")
+                    else:
+                        y_t = conv_pass(blk, chunk, turn_psum, "turn")
+                    nc.vector.bn_stats(out=stats[:, chunk, blk, :], in_=y_t[:])
+
+            w_grouped = turn_k_onto_partitions(w_sb)
+            grouped[0] = turn_k_onto_partitions(ctx_sb[0])
+            nc.vector.quantize_mx(out=w_codes[:].bitcast(FP8X4), scales=w_scales[:], in_=w_grouped[:])
+            grouped[1] = turn_k_onto_partitions(ctx_sb[1])
+            quantise(0)
+            multiply(0)
+
+            bn_turned = turn_psum.tile([P, P], BF16, name="bn_turned", tag="turn")
+            nc.tensor.transpose(out=bn_turned[:], in_=bn_rows[:], identity=ident_bf[:])
+            bn_cols = const.tile([P, 2 * CHUNKS], F32, name="bn_cols")
+            nc.vector.tensor_copy(out=bn_cols[:], in_=bn_turned[:, 0 : 2 * CHUNKS])
+            ln_both = gain_psum.tile([P, 2, D], BF16, name="ln_both")
+            nc.tensor.matmul(out=ln_both[:, 0, :], lhsT=ones[:], rhs=ln_rows[:, 0, :], start=True, stop=True)
+            nc.tensor.matmul(out=ln_both[:, 1, :], lhsT=ones[:], rhs=ln_rows[:, 1, :], start=True, stop=True)
+            ln_gain = ln_both[:, 0, :]
+            ln_bias = ln_both[:, 1, :]
+            slope = const.tile([P, 1], F32, name="slope")
+            nc.vector.tensor_copy(out=slope[:], in_=slope_bf[:])
+            one_minus_slope = const.tile([P, 1], F32, name="one_minus_slope")
+            nc.vector.tensor_scalar(
+                out=one_minus_slope[:], in0=slope[:], scalar1=-1.0, scalar2=1.0, op0=ALU.mult, op1=ALU.add
+            )
+            flip = const.tile([P, 1], F32, name="flip")
+            nc.vector.tensor_scalar(out=flip[:], in0=one_minus_slope[:], scalar1=0.0, scalar2=2.0, op0=ALU.is_ge, op1=ALU.mult)
+            nc.vector.tensor_scalar_add(out=flip[:], in0=flip[:], scalar1=-1.0)
+            line_factor = const.tile([P, 1], F32, name="line_factor")
+            nc.vector.tensor_mul(out=line_factor[:], in0=slope[:], in1=flip[:])
+            relu_factor = const.tile([P, 1], F32, name="relu_factor")
+            nc.vector.tensor_mul(out=relu_factor[:], in0=one_minus_slope[:], in1=flip[:])
+
+            for blk in range(1, BLOCKS):
+                multiply(blk)
+
+        sum_pool = stack.enter_context(tc.tile_pool(name="sums", bufs=1))
+        sums = []
+        for blk in range(BLOCKS):
+            sum_t = sum_pool.tile([P, TILES, D], F32, name="sum_t%d" % blk)
+            for j in range(TILES):
+                nc.gpsimd.tensor_tensor(out=sum_t[:, j, :], in0=x_sb[blk][:, j, :], in1=res_sb[blk][:, j, :], op=ALU.add)
+            sums.append(sum_t)
+
+        mean_var = const.tile([P, CHUNKS, 2], F32, name="mean_var")
+        for chunk in range(CHUNKS):
+            nc.vector.bn_aggr(out=mean_var[:, chunk, :], in_=stats[:, chunk, :, :].rearrange("p b s -> p (b s)"))
+        bn_rstd = const.tile([P, CHUNKS], F32, name="bn_rstd")
+        nc.scalar.activation(
+            out=bn_rstd[:], in_=mean_var[:, :, 1], func=ACT.Abs_reciprocal_sqrt, bias=eps_bn[:], scale=1.0
+        )
+        bn_scale = const.tile([P, CHUNKS], F32, name="bn_scale")
+        nc.vector.tensor_mul(out=bn_scale[:], in0=bn_cols[:, 0:CHUNKS], in1=bn_rstd[:])
+        bn_shift = const.tile([P, CHUNKS], F32, name="bn_shift")
+        nc.vector.tensor_mul(out=bn_shift[:], in0=mean_var[:, :, 0], in1=bn_scale[:])
+        nc.vector.tensor_sub(out=bn_shift[:], in0=bn_cols[:, CHUNKS : 2 * CHUNKS], in1=bn_shift[:])
+        line_scale = const.tile([P, CHUNKS], F32, name="line_scale")
+        nc.vector.tensor_scalar_mul(out=line_scale[:], in0=bn_scale[:], scalar1=line_factor[:])
+        line_shift = const.tile([P, CHUNKS], F32, name="line_shift")
+        nc.vector.tensor_scalar_mul(out=line_shift[:], in0=bn_shift[:], scalar1=line_factor[:])
+        relu_scale = const.tile([P, CHUNKS], F32, name="relu_scale")
+        nc.vector.tensor_scalar_mul(out=relu_scale[:], in0=bn_scale[:], scalar1=relu_factor[:])
+        relu_shift = const.tile([P, CHUNKS], F32, name="relu_shift")
+        nc.vector.tensor_scalar_mul(out=relu_shift[:], in0=bn_shift[:], scalar1=relu_factor[:])
+        neg_relu_shift = const.tile([P, CHUNKS], F32, name="neg_relu_shift")
+        nc.vector.tensor_scalar_mul(out=neg_relu_shift[:], in0=relu_shift[:], scalar1=-1.0)
+        both_shifts = const.tile([P, CHUNKS], F32, name="both_shifts")
+        nc.vector.tensor_add(out=both_shifts[:], in0=line_shift[:], in1=relu_shift[:])
+
+        lines, relus, turned_back, row_sums, neg_means, row_rstds = {}, {}, {}, {}, {}, {}
+
+        def affine(blk, chunk):
+            col = slice(chunk, chunk + 1)
+            y_t = conv_pass(blk, chunk, y_psum, "y")
+            line = branch.tile([P, TILES * P], F32, name="line")
+            relu = branch.tile([P, TILES * P], F32, name="relu")
+            if blk < HELPED and chunk % 2 == 1:
+                nc.vector.tensor_scalar(
+                    out=line[:], in0=y_t[:], scalar1=line_scale[:, col], scalar2=both_shifts[:, col],
+                    op0=ALU.mult, op1=ALU.add,
+                )
+                nc.vector.tensor_scalar(
+                    out=relu[:], in0=y_t[:], scalar1=relu_scale[:, col], scalar2=neg_relu_shift[:, col],
+                    op0=ALU.mult, op1=ALU.max,
+                )
+            else:
+                nc.scalar.activation(
+                    out=line[:], in_=y_t[:], func=ACT.Identity, bias=line_shift[:, col], scale=line_scale[:, col]
+                )
+                nc.scalar.activation(
+                    out=relu[:], in_=y_t[:], func=ACT.Relu, bias=relu_shift[:, col], scale=relu_scale[:, col]
+                )
+            lines[(blk, chunk)] = line
+            relus[(blk, chunk)] = relu
+
+        def turn_back(blk, j):
+            back = turn_psum.tile([P, D], F32, name="back", tag="turn")
+            for chunk in range(CHUNKS):
+                for term, first in ((lines[(blk, chunk)], True), (relus[(blk, chunk)], False)):
+                    nc.tensor.matmul(
+                        out=back[:, chunk * P : (chunk + 1) * P], lhsT=term[:, j * P : (j + 1) * P],
+                        rhs=ident_f32[:], is_transpose=True, start=first, stop=not first,
+                    )
+            turned_back[(blk, j)] = back
+
+        def add_streams(blk, j):
+            if j == 0:
+                row_sums[blk] = small.tile([P, TILES], F32, name="row_sum")
+            nc.vector.scalar_tensor_tensor(
+                out=sums[blk][:, j, :], in0=turned_back[(blk, j)][:], scalar=flip[:], in1=sums[blk][:, j, :],
+                op0=ALU.mult, op1=ALU.add, accum_out=row_sums[blk][:, j : j + 1],
+            )
+
+        def deviation(blk):
+            neg_mean = small.tile([P, TILES], F32, name="neg_mean")
+            nc.scalar.mul(out=neg_mean[:], in_=row_sums[blk][:], mul=-1.0 / D)
+            square_sum = small.tile([P, TILES], F32, name="square_sum")
+            for j in range(TILES):
+                unread = scrap.tile([P, D], BF16, name="unread")
+                nc.scalar.activation(
+                    out=unread[:], in_=sums[blk][:, j, :], func=ACT.Square, bias=neg_mean[:, j : j + 1], scale=1.0,
+                    accum_out=square_sum[:, j : j + 1],
+                )
+            row_rstd = small.tile([P, TILES], F32, name="row_rstd")
+            nc.scalar.activation(
+                out=row_rstd[:], in_=square_sum[:], func=ACT.Abs_reciprocal_sqrt, bias=eps_ln[:], scale=1.0 / D
+            )
+            neg_means[blk] = neg_mean
+            row_rstds[blk] = row_rstd
+
+        def normalise(blk):
+            l_rows, b_rows = block_rows(blk)
+            first_b = (blk % (B // TILES)) * TILES
+            row_rstd = row_rstds[blk]
+            for j in range(TILES):
+                nc.vector.scalar_tensor_tensor(
+                    out=sums[blk][:, j, :], in0=sums[blk][:, j, :], scalar=neg_means[blk][:, j : j + 1], in1=ln_gain,
+                    op0=ALU.add, op1=ALU.mult,
+                )
+            for j in range(TILES):
+                nc.vector.scalar_tensor_tensor(
+                    out=sums[blk][:, j, :], in0=sums[blk][:, j, :], scalar=row_rstd[:, j : j + 1], in1=ln_bias,
+                    op0=ALU.mult, op1=ALU.add,
+                )
+                nc.sync.dma_start(out=out[l_rows, first_b + j : first_b + j + 1, :], in_=sums[blk][:, j : j + 1, :])
+
+        for step in range(-3, BLOCKS):
+            for half in range(2):
+                pair = (2 * half, 2 * half + 1)
+                if 0 <= step + 3 < BLOCKS:
+                    for chunk in pair:
+                        affine(step + 3, chunk)
+                if half == 0 and 0 <= step + 1 < BLOCKS:
+                    for j in range(TILES):
+                        add_streams(step + 1, j)
+                    deviation(step + 1)
+                if 0 <= step + 2 < BLOCKS:
+                    for j in pair:
+                        turn_back(step + 2, j)
+            if 0 <= step:
+                normalise(step)

@@ -19,7 +19,7 @@ TILES = 4
 BLOCKS = L * B // (TILES * P)
 CHUNKS = D // P
 WORDS = D // 2
-HELPED = 2
+LATE = (BLOCKS - 2, BLOCKS - 1)
 FLOPS = 2 * L * B * D * D
 
 
@@ -29,7 +29,7 @@ def tile_coattention_pb_t_kernel(tc, x, res_a, ctx_v, W_v, bn_v_g, bn_v_b, prelu
         stack.enter_context(tc.manual_schedule())
         const = stack.enter_context(tc.tile_pool(name="const", bufs=1))
         keep = stack.enter_context(tc.tile_pool(name="keep", bufs=1))
-        branch = stack.enter_context(tc.tile_pool(name="branch", bufs=2 * CHUNKS))
+        branch = stack.enter_context(tc.tile_pool(name="branch", bufs=4))
         scrap = stack.enter_context(tc.tile_pool(name="scrap", bufs=4))
         small = stack.enter_context(tc.tile_pool(name="small", bufs=3))
         gain_psum = stack.enter_context(tc.psum_pool(name="gain_psum", bufs=1))
@@ -151,31 +151,43 @@ def tile_coattention_pb_t_kernel(tc, x, res_a, ctx_v, W_v, bn_v_g, bn_v_b, prelu
             quantise(0)
             multiply(0)
 
+            for blk in range(1, LATE[0]):
+                multiply(blk)
+            quantise(LATE[1])
+
             bn_turned = turn_psum.tile([P, P], BF16, name="bn_turned", tag="turn")
             nc.tensor.transpose(out=bn_turned[:], in_=bn_rows[:], identity=ident_bf[:])
             bn_cols = const.tile([P, 2 * CHUNKS], F32, name="bn_cols")
-            nc.vector.tensor_copy(out=bn_cols[:], in_=bn_turned[:, 0 : 2 * CHUNKS])
+            nc.scalar.copy(out=bn_cols[:], in_=bn_turned[:, 0 : 2 * CHUNKS])
             ln_both = gain_psum.tile([P, 2, D], BF16, name="ln_both")
             nc.tensor.matmul(out=ln_both[:, 0, :], lhsT=ones[:], rhs=ln_rows[:, 0, :], start=True, stop=True)
             nc.tensor.matmul(out=ln_both[:, 1, :], lhsT=ones[:], rhs=ln_rows[:, 1, :], start=True, stop=True)
             ln_gain = ln_both[:, 0, :]
             ln_bias = ln_both[:, 1, :]
-            slope = const.tile([P, 1], F32, name="slope")
-            nc.vector.tensor_copy(out=slope[:], in_=slope_bf[:])
             one_minus_slope = const.tile([P, 1], F32, name="one_minus_slope")
             nc.vector.tensor_scalar(
-                out=one_minus_slope[:], in0=slope[:], scalar1=-1.0, scalar2=1.0, op0=ALU.mult, op1=ALU.add
+                out=one_minus_slope[:], in0=slope_bf[:], scalar1=-1.0, scalar2=1.0, op0=ALU.mult, op1=ALU.add
             )
             flip = const.tile([P, 1], F32, name="flip")
-            nc.vector.tensor_scalar(out=flip[:], in0=one_minus_slope[:], scalar1=0.0, scalar2=2.0, op0=ALU.is_ge, op1=ALU.mult)
+            nc.vector.tensor_scalar(
+                out=flip[:], in0=one_minus_slope[:], scalar1=0.0, scalar2=2.0, op0=ALU.is_ge, op1=ALU.mult
+            )
             nc.vector.tensor_scalar_add(out=flip[:], in0=flip[:], scalar1=-1.0)
-            line_factor = const.tile([P, 1], F32, name="line_factor")
-            nc.vector.tensor_mul(out=line_factor[:], in0=slope[:], in1=flip[:])
-            relu_factor = const.tile([P, 1], F32, name="relu_factor")
-            nc.vector.tensor_mul(out=relu_factor[:], in0=one_minus_slope[:], in1=flip[:])
-
-            for blk in range(1, BLOCKS):
-                multiply(blk)
+            parts = const.tile([P, 6], F32, name="parts")
+            nc.scalar.activation(out=parts[:, 0:1], in_=slope_bf[:], func=ACT.Copy, scale=flip[:])
+            nc.scalar.activation(out=parts[:, 1:2], in_=one_minus_slope[:], func=ACT.Copy, scale=flip[:])
+            nc.scalar.mul(out=parts[:, 2:4], in_=parts[:, 0:2], mul=-1.0)
+            nc.scalar.copy(out=parts[:, 4:5], in_=parts[:, 1:2])
+            nc.scalar.mul(out=parts[:, 5:6], in_=flip[:], mul=-1.0)
+            minus_parts = const.tile([P, 4], F32, name="minus_parts")
+            nc.scalar.mul(out=minus_parts[:], in_=parts[:, 2:6], mul=-1.0)
+            factors = const.tile([P, CHUNKS, 6], F32, name="factors")
+            constants = const.tile([P, CHUNKS, 4], F32, name="constants")
+            for chunk in range(CHUNKS):
+                gamma = bn_cols[:, chunk : chunk + 1]
+                beta = bn_cols[:, CHUNKS + chunk : CHUNKS + chunk + 1]
+                nc.scalar.activation(out=factors[:, chunk, :], in_=parts[:], func=ACT.Copy, scale=gamma)
+                nc.scalar.activation(out=constants[:, chunk, :], in_=minus_parts[:], func=ACT.Copy, scale=beta)
 
         sum_pool = stack.enter_context(tc.tile_pool(name="sums", bufs=1))
         sums = []
@@ -186,52 +198,47 @@ def tile_coattention_pb_t_kernel(tc, x, res_a, ctx_v, W_v, bn_v_g, bn_v_b, prelu
             sums.append(sum_t)
 
         mean_var = const.tile([P, CHUNKS, 2], F32, name="mean_var")
-        for chunk in range(CHUNKS):
-            nc.vector.bn_aggr(out=mean_var[:, chunk, :], in_=stats[:, chunk, :, :].rearrange("p b s -> p (b s)"))
         bn_rstd = const.tile([P, CHUNKS], F32, name="bn_rstd")
-        nc.scalar.activation(
-            out=bn_rstd[:], in_=mean_var[:, :, 1], func=ACT.Abs_reciprocal_sqrt, bias=eps_bn[:], scale=1.0
-        )
-        bn_scale = const.tile([P, CHUNKS], F32, name="bn_scale")
-        nc.vector.tensor_mul(out=bn_scale[:], in0=bn_cols[:, 0:CHUNKS], in1=bn_rstd[:])
-        bn_shift = const.tile([P, CHUNKS], F32, name="bn_shift")
-        nc.vector.tensor_mul(out=bn_shift[:], in0=mean_var[:, :, 0], in1=bn_scale[:])
-        nc.vector.tensor_sub(out=bn_shift[:], in0=bn_cols[:, CHUNKS : 2 * CHUNKS], in1=bn_shift[:])
-        line_scale = const.tile([P, CHUNKS], F32, name="line_scale")
-        nc.vector.tensor_scalar_mul(out=line_scale[:], in0=bn_scale[:], scalar1=line_factor[:])
-        line_shift = const.tile([P, CHUNKS], F32, name="line_shift")
-        nc.vector.tensor_scalar_mul(out=line_shift[:], in0=bn_shift[:], scalar1=line_factor[:])
-        relu_scale = const.tile([P, CHUNKS], F32, name="relu_scale")
-        nc.vector.tensor_scalar_mul(out=relu_scale[:], in0=bn_scale[:], scalar1=relu_factor[:])
-        relu_shift = const.tile([P, CHUNKS], F32, name="relu_shift")
-        nc.vector.tensor_scalar_mul(out=relu_shift[:], in0=bn_shift[:], scalar1=relu_factor[:])
-        neg_relu_shift = const.tile([P, CHUNKS], F32, name="neg_relu_shift")
-        nc.vector.tensor_scalar_mul(out=neg_relu_shift[:], in0=relu_shift[:], scalar1=-1.0)
-        both_shifts = const.tile([P, CHUNKS], F32, name="both_shifts")
-        nc.vector.tensor_add(out=both_shifts[:], in0=line_shift[:], in1=relu_shift[:])
+        scales = const.tile([P, CHUNKS, 6], F32, name="scales")
+        shifts = const.tile([P, CHUNKS, 4], F32, name="shifts")
+
+        def aggregate(chunk):
+            nc.vector.bn_aggr(out=mean_var[:, chunk, :], in_=stats[:, chunk, :, :].rearrange("p b s -> p (b s)"))
+            nc.scalar.activation(
+                out=bn_rstd[:, chunk : chunk + 1], in_=mean_var[:, chunk, 1:2], func=ACT.Abs_reciprocal_sqrt,
+                bias=eps_bn[:], scale=1.0,
+            )
+
+        def prepare(chunk):
+            nc.vector.tensor_scalar_mul(
+                out=scales[:, chunk, :], in0=factors[:, chunk, :], scalar1=bn_rstd[:, chunk : chunk + 1]
+            )
+            nc.vector.scalar_tensor_tensor(
+                out=shifts[:, chunk, :], in0=scales[:, chunk, 2:6], scalar=mean_var[:, chunk, 0:1],
+                in1=constants[:, chunk, :], op0=ALU.mult, op1=ALU.add,
+            )
 
         lines, relus, turned_back, row_sums, neg_means, row_rstds = {}, {}, {}, {}, {}, {}
 
-        def affine(blk, chunk):
-            col = slice(chunk, chunk + 1)
+        def affine(blk, chunk, on_vector=False):
             y_t = conv_pass(blk, chunk, y_psum, "y")
-            line = branch.tile([P, TILES * P], F32, name="line")
-            relu = branch.tile([P, TILES * P], F32, name="relu")
-            if blk < HELPED and chunk % 2 == 1:
+            line = branch.tile([P, TILES * P], F32, name="line%d" % chunk)
+            relu = branch.tile([P, TILES * P], F32, name="relu%d" % chunk)
+            line_scale = scales[:, chunk, 0:1]
+            relu_scale = scales[:, chunk, 1:2]
+            if on_vector:
                 nc.vector.tensor_scalar(
-                    out=line[:], in0=y_t[:], scalar1=line_scale[:, col], scalar2=both_shifts[:, col],
-                    op0=ALU.mult, op1=ALU.add,
+                    out=line[:], in0=y_t[:], scalar1=line_scale, scalar2=shifts[:, chunk, 3:4], op0=ALU.mult, op1=ALU.add
                 )
                 nc.vector.tensor_scalar(
-                    out=relu[:], in0=y_t[:], scalar1=relu_scale[:, col], scalar2=neg_relu_shift[:, col],
-                    op0=ALU.mult, op1=ALU.max,
+                    out=relu[:], in0=y_t[:], scalar1=relu_scale, scalar2=shifts[:, chunk, 2:3], op0=ALU.mult, op1=ALU.max
                 )
             else:
                 nc.scalar.activation(
-                    out=line[:], in_=y_t[:], func=ACT.Identity, bias=line_shift[:, col], scale=line_scale[:, col]
+                    out=line[:], in_=y_t[:], func=ACT.Identity, bias=shifts[:, chunk, 0:1], scale=line_scale
                 )
                 nc.scalar.activation(
-                    out=relu[:], in_=y_t[:], func=ACT.Relu, bias=relu_shift[:, col], scale=relu_scale[:, col]
+                    out=relu[:], in_=y_t[:], func=ACT.Relu, bias=shifts[:, chunk, 1:2], scale=relu_scale
                 )
             lines[(blk, chunk)] = line
             relus[(blk, chunk)] = relu
@@ -287,18 +294,43 @@ def tile_coattention_pb_t_kernel(tc, x, res_a, ctx_v, W_v, bn_v_g, bn_v_b, prelu
                 )
                 nc.sync.dma_start(out=out[l_rows, first_b + j : first_b + j + 1, :], in_=sums[blk][:, j : j + 1, :])
 
-        for step in range(-3, BLOCKS):
+        last = CHUNKS - 1
+        for chunk in range(CHUNKS):
+            for blk in LATE:
+                nc.vector.bn_stats(out=stats[:, chunk, blk, :], in_=conv_pass(blk, chunk, turn_psum, "turn")[:])
+            if 0 < chunk:
+                prepare(chunk - 1)
+            aggregate(chunk)
+            if 0 < chunk:
+                affine(0, chunk - 1)
+        prepare(last)
+        affine(0, last, on_vector=True)
+        affine(1, last, on_vector=True)
+        affine(1, 0)
+        for half in range(2):
+            for j in (2 * half, 2 * half + 1):
+                turn_back(0, j)
+            affine(1, 1 + half)
+        for j in range(TILES):
+            add_streams(0, j)
+        deviation(0)
+        affine(2, last, on_vector=True)
+        for j in range(TILES):
+            turn_back(1, j)
+        affine(2, 0)
+
+        for step in range(BLOCKS):
+            if step + 1 < BLOCKS:
+                for j in range(TILES):
+                    add_streams(step + 1, j)
             for half in range(2):
-                pair = (2 * half, 2 * half + 1)
-                if 0 <= step + 3 < BLOCKS:
-                    for chunk in pair:
-                        affine(step + 3, chunk)
-                if half == 0 and 0 <= step + 1 < BLOCKS:
-                    for j in range(TILES):
-                        add_streams(step + 1, j)
+                blk = step + 2 + half
+                if blk < BLOCKS:
+                    for chunk in (2 - 2 * half, 3 - 2 * half) if step else ((1, 2) if half == 0 else (0, 1)):
+                        affine(blk, chunk)
+                if half == 0 and step + 1 < BLOCKS:
                     deviation(step + 1)
-                if 0 <= step + 2 < BLOCKS:
-                    for j in pair:
+                if step + 2 < BLOCKS:
+                    for j in (2 * half, 2 * half + 1):
                         turn_back(step + 2, j)
-            if 0 <= step:
-                normalise(step)
+            normalise(step)

@@ -20,6 +20,10 @@ BLOCKS = L * B // (TILES * P)
 CHUNKS = D // P
 WORDS = D // 2
 LATE = (BLOCKS - 2, BLOCKS - 1)
+LAST = CHUNKS - 1
+ON_SCALAR = range(1, 5)
+KEEP = [blk for blk in range(BLOCKS) if blk not in ON_SCALAR]
+REPEAT = 2
 FLOPS = 2 * L * B * D * D
 
 
@@ -93,7 +97,7 @@ def tile_coattention_pb_t_kernel(tc, x, res_a, ctx_v, W_v, bn_v_g, bn_v_b, prelu
             ctx_codes = keep.tile([P, BLOCKS, TILES * P], U32, name="ctx_codes", align_bytes=64)
             ctx_scales = keep.tile([P, BLOCKS, TILES * P], U8, name="ctx_scales", align_bytes=64)
 
-            def turn_k_onto_partitions(rows_sb):
+            def turn_k_onto_partitions(rows_sb, vector_helps=False):
                 words = rows_sb[:].bitcast(F32)
                 grouped = stage.tile([P, TILES * P * 4], BF16, name="grouped", align_bytes=64)
                 grouped_words = grouped[:].bitcast(F32).rearrange("p (c u) -> p c u", u=2)
@@ -105,27 +109,49 @@ def tile_coattention_pb_t_kernel(tc, x, res_a, ctx_v, W_v, bn_v_g, bn_v_b, prelu
                             nc.tensor.transpose(
                                 out=turned[:, u, i * P : (i + 1) * P], in_=words[:, row_words + u : row_words + WORDS : 2], identity=ident_f32[:]
                             )
-                    nc.scalar.copy(
-                        out=grouped_words[:, 2 * pair * P : 2 * (pair + 1) * P, :], in_=turned[:].rearrange("p u r -> p r u")
-                    )
+                    copied = grouped_words[:, 2 * pair * P : 2 * (pair + 1) * P, :]
+                    if vector_helps and pair == 1:
+                        nc.vector.tensor_copy(out=copied, in_=turned[:].rearrange("p u r -> p r u"))
+                    else:
+                        nc.scalar.copy(out=copied, in_=turned[:].rearrange("p u r -> p r u"))
                 return grouped
 
-            def conv_pass(blk, chunk, bank_pool, bank_tag):
+            def conv_pass(blk, chunk, bank_pool, bank_tag, repeat=1):
                 y_t = bank_pool.tile([P, TILES * P], F32, name="y_t", tag=bank_tag)
                 c_cols = slice(chunk * P, (chunk + 1) * P)
-                nc.tensor.matmul_mx(
-                    out=y_t[:],
-                    lhsT=w_codes[:, c_cols].bitcast(FP8X4),
-                    lhsT_scale=w_scales[:, c_cols],
-                    rhs=ctx_codes[:, blk, :].bitcast(FP8X4),
-                    rhs_scale=ctx_scales[:, blk, :],
-                    start=True,
-                    stop=True,
-                )
+                for again in range(repeat):
+                    nc.tensor.matmul_mx(
+                        out=y_t[:],
+                        lhsT=w_codes[:, c_cols].bitcast(FP8X4),
+                        lhsT_scale=w_scales[:, c_cols],
+                        rhs=ctx_codes[:, blk, :].bitcast(FP8X4),
+                        rhs_scale=ctx_scales[:, blk, :],
+                        start=True,
+                        stop=True,
+                    )
                 return y_t
 
             grouped = {}
-            stats = keep.tile([P, CHUNKS, BLOCKS, 6], F32, name="stats")
+            stats = keep.tile([P, CHUNKS, BLOCKS * 6], F32, name="stats")
+            pivot_sums = keep.tile([P, 2, len(ON_SCALAR)], F32, name="pivot_sums")
+            neg_pivot = keep.tile([P, 1], F32, name="neg_pivot")
+
+            def take_statistics(blk, chunk, y_t):
+                if chunk < LAST:
+                    nc.vector.bn_stats(out=stats[:, chunk, blk * 6 : (blk + 1) * 6], in_=y_t[:])
+                elif blk in ON_SCALAR:
+                    if blk == ON_SCALAR[0]:
+                        nc.scalar.mul(out=neg_pivot[:], in_=stats[:, LAST, 1:2], mul=-1.0)
+                    for power, func in enumerate((ACT.Identity, ACT.Square)):
+                        unread = scrap.tile([P, D], BF16, name="unread")
+                        column = ON_SCALAR.index(blk)
+                        nc.scalar.activation(
+                            out=unread[:], in_=y_t[:], func=func, bias=neg_pivot[:], scale=1.0,
+                            accum_out=pivot_sums[:, power, column : column + 1],
+                        )
+                else:
+                    place = KEEP.index(blk)
+                    nc.vector.bn_stats(out=stats[:, chunk, place * 6 : (place + 1) * 6], in_=y_t[:])
 
             def quantise(blk):
                 nc.vector.quantize_mx(
@@ -142,10 +168,10 @@ def tile_coattention_pb_t_kernel(tc, x, res_a, ctx_v, W_v, bn_v_g, bn_v_b, prelu
                         y_t = conv_pass(blk, chunk, y_psum, "y")
                     else:
                         y_t = conv_pass(blk, chunk, turn_psum, "turn")
-                    nc.vector.bn_stats(out=stats[:, chunk, blk, :], in_=y_t[:])
+                    take_statistics(blk, chunk, y_t)
 
-            w_grouped = turn_k_onto_partitions(w_sb)
-            grouped[0] = turn_k_onto_partitions(ctx_sb[0])
+            w_grouped = turn_k_onto_partitions(w_sb, vector_helps=True)
+            grouped[0] = turn_k_onto_partitions(ctx_sb[0], vector_helps=True)
             nc.vector.quantize_mx(out=w_codes[:].bitcast(FP8X4), scales=w_scales[:], in_=w_grouped[:])
             grouped[1] = turn_k_onto_partitions(ctx_sb[1])
             quantise(0)
@@ -165,22 +191,22 @@ def tile_coattention_pb_t_kernel(tc, x, res_a, ctx_v, W_v, bn_v_g, bn_v_b, prelu
             ln_gain = ln_both[:, 0, :]
             ln_bias = ln_both[:, 1, :]
             one_minus_slope = const.tile([P, 1], F32, name="one_minus_slope")
-            nc.vector.tensor_scalar(
+            nc.gpsimd.tensor_scalar(
                 out=one_minus_slope[:], in0=slope_bf[:], scalar1=-1.0, scalar2=1.0, op0=ALU.mult, op1=ALU.add
             )
             flip = const.tile([P, 1], F32, name="flip")
-            nc.vector.tensor_scalar(
+            nc.gpsimd.tensor_scalar(
                 out=flip[:], in0=one_minus_slope[:], scalar1=0.0, scalar2=2.0, op0=ALU.is_ge, op1=ALU.mult
             )
-            nc.vector.tensor_scalar_add(out=flip[:], in0=flip[:], scalar1=-1.0)
+            nc.gpsimd.tensor_scalar(out=flip[:], in0=flip[:], scalar1=1.0, scalar2=None, op0=ALU.subtract)
             parts = const.tile([P, 6], F32, name="parts")
-            nc.scalar.activation(out=parts[:, 0:1], in_=slope_bf[:], func=ACT.Copy, scale=flip[:])
-            nc.scalar.activation(out=parts[:, 1:2], in_=one_minus_slope[:], func=ACT.Copy, scale=flip[:])
-            nc.scalar.mul(out=parts[:, 2:4], in_=parts[:, 0:2], mul=-1.0)
-            nc.scalar.copy(out=parts[:, 4:5], in_=parts[:, 1:2])
-            nc.scalar.mul(out=parts[:, 5:6], in_=flip[:], mul=-1.0)
+            nc.gpsimd.tensor_tensor(out=parts[:, 0:1], in0=flip[:], in1=slope_bf[:], op=ALU.mult)
+            nc.gpsimd.tensor_tensor(out=parts[:, 1:2], in0=flip[:], in1=one_minus_slope[:], op=ALU.mult)
+            nc.gpsimd.tensor_scalar(out=parts[:, 2:4], in0=parts[:, 0:2], scalar1=-1.0, scalar2=None, op0=ALU.mult)
+            nc.gpsimd.tensor_copy(out=parts[:, 4:5], in_=parts[:, 1:2])
+            nc.gpsimd.tensor_scalar(out=parts[:, 5:6], in0=flip[:], scalar1=-1.0, scalar2=None, op0=ALU.mult)
             minus_parts = const.tile([P, 4], F32, name="minus_parts")
-            nc.scalar.mul(out=minus_parts[:], in_=parts[:, 2:6], mul=-1.0)
+            nc.gpsimd.tensor_scalar(out=minus_parts[:], in0=parts[:, 2:6], scalar1=-1.0, scalar2=None, op0=ALU.mult)
             factors = const.tile([P, CHUNKS, 6], F32, name="factors")
             constants = const.tile([P, CHUNKS, 4], F32, name="constants")
             for chunk in range(CHUNKS):
@@ -188,6 +214,25 @@ def tile_coattention_pb_t_kernel(tc, x, res_a, ctx_v, W_v, bn_v_g, bn_v_b, prelu
                 beta = bn_cols[:, CHUNKS + chunk : CHUNKS + chunk + 1]
                 nc.scalar.activation(out=factors[:, chunk, :], in_=parts[:], func=ACT.Copy, scale=gamma)
                 nc.scalar.activation(out=constants[:, chunk, :], in_=minus_parts[:], func=ACT.Copy, scale=beta)
+
+            count = len(ON_SCALAR) * TILES * P
+            triple = stats[:, LAST, len(KEEP) * 6 : len(KEEP) * 6 + 3]
+            nc.gpsimd.memset(triple[:, 0:1], float(count))
+            totals = const.tile([P, 2], F32, name="totals")
+            for power in range(2):
+                unread_sums = const.tile([P, len(ON_SCALAR)], F32, name="unread_sums%d" % power)
+                nc.scalar.activation(
+                    out=unread_sums[:], in_=pivot_sums[:, power, :], func=ACT.Identity, scale=1.0,
+                    accum_out=totals[:, power : power + 1],
+                )
+            neg_offset = const.tile([P, 1], F32, name="neg_offset")
+            nc.scalar.mul(out=neg_offset[:], in_=totals[:, 0:1], mul=-1.0 / count)
+            nc.scalar.activation(
+                out=triple[:, 1:2], in_=neg_offset[:], func=ACT.Identity, scale=-1.0, bias=stats[:, LAST, 1:2]
+            )
+            nc.scalar.activation(
+                out=triple[:, 2:3], in_=totals[:, 0:1], func=ACT.Identity, scale=neg_offset[:], bias=totals[:, 1:2]
+            )
 
         sum_pool = stack.enter_context(tc.tile_pool(name="sums", bufs=1))
         sums = []
@@ -203,7 +248,8 @@ def tile_coattention_pb_t_kernel(tc, x, res_a, ctx_v, W_v, bn_v_g, bn_v_b, prelu
         shifts = const.tile([P, CHUNKS, 4], F32, name="shifts")
 
         def aggregate(chunk):
-            nc.vector.bn_aggr(out=mean_var[:, chunk, :], in_=stats[:, chunk, :, :].rearrange("p b s -> p (b s)"))
+            values = len(KEEP) * 6 + 3 if chunk == LAST else BLOCKS * 6
+            nc.vector.bn_aggr(out=mean_var[:, chunk, :], in_=stats[:, chunk, 0:values])
             nc.scalar.activation(
                 out=bn_rstd[:, chunk : chunk + 1], in_=mean_var[:, chunk, 1:2], func=ACT.Abs_reciprocal_sqrt,
                 bias=eps_bn[:], scale=1.0,
@@ -221,7 +267,7 @@ def tile_coattention_pb_t_kernel(tc, x, res_a, ctx_v, W_v, bn_v_g, bn_v_b, prelu
         lines, relus, turned_back, row_sums, neg_means, row_rstds = {}, {}, {}, {}, {}, {}
 
         def affine(blk, chunk, on_vector=False):
-            y_t = conv_pass(blk, chunk, y_psum, "y")
+            y_t = conv_pass(blk, chunk, y_psum, "y", REPEAT)
             line = branch.tile([P, TILES * P], F32, name="line%d" % chunk)
             relu = branch.tile([P, TILES * P], F32, name="relu%d" % chunk)
             line_scale = scales[:, chunk, 0:1]
@@ -278,59 +324,65 @@ def tile_coattention_pb_t_kernel(tc, x, res_a, ctx_v, W_v, bn_v_g, bn_v_b, prelu
             neg_means[blk] = neg_mean
             row_rstds[blk] = row_rstd
 
-        def normalise(blk):
-            l_rows, b_rows = block_rows(blk)
-            first_b = (blk % (B // TILES)) * TILES
-            row_rstd = row_rstds[blk]
+        def take_off_means(blk):
             for j in range(TILES):
                 nc.vector.scalar_tensor_tensor(
                     out=sums[blk][:, j, :], in0=sums[blk][:, j, :], scalar=neg_means[blk][:, j : j + 1], in1=ln_gain,
                     op0=ALU.add, op1=ALU.mult,
                 )
+
+        def scale_and_store(blk):
+            l_rows, b_rows = block_rows(blk)
+            first_b = (blk % (B // TILES)) * TILES
             for j in range(TILES):
                 nc.vector.scalar_tensor_tensor(
-                    out=sums[blk][:, j, :], in0=sums[blk][:, j, :], scalar=row_rstd[:, j : j + 1], in1=ln_bias,
+                    out=sums[blk][:, j, :], in0=sums[blk][:, j, :], scalar=row_rstds[blk][:, j : j + 1], in1=ln_bias,
                     op0=ALU.mult, op1=ALU.add,
                 )
                 nc.sync.dma_start(out=out[l_rows, first_b + j : first_b + j + 1, :], in_=sums[blk][:, j : j + 1, :])
 
-        last = CHUNKS - 1
         for chunk in range(CHUNKS):
             for blk in LATE:
-                nc.vector.bn_stats(out=stats[:, chunk, blk, :], in_=conv_pass(blk, chunk, turn_psum, "turn")[:])
+                take_statistics(blk, chunk, conv_pass(blk, chunk, turn_psum, "turn"))
             if 0 < chunk:
                 prepare(chunk - 1)
             aggregate(chunk)
             if 0 < chunk:
                 affine(0, chunk - 1)
-        prepare(last)
-        affine(0, last, on_vector=True)
-        affine(1, last, on_vector=True)
+        prepare(LAST)
+        affine(0, LAST, on_vector=True)
+        affine(1, LAST, on_vector=True)
         affine(1, 0)
+        affine(1, 1)
         for half in range(2):
             for j in (2 * half, 2 * half + 1):
                 turn_back(0, j)
-            affine(1, 1 + half)
+            if half == 0:
+                affine(1, 2)
         for j in range(TILES):
             add_streams(0, j)
         deviation(0)
-        affine(2, last, on_vector=True)
+        affine(2, LAST, on_vector=True)
+        affine(2, 0)
         for j in range(TILES):
             turn_back(1, j)
-        affine(2, 0)
+        affine(2, 1)
+        for j in range(TILES):
+            add_streams(1, j)
+        affine(2, 2)
 
         for step in range(BLOCKS):
-            if step + 1 < BLOCKS:
-                for j in range(TILES):
-                    add_streams(step + 1, j)
-            for half in range(2):
-                blk = step + 2 + half
-                if blk < BLOCKS:
-                    for chunk in (2 - 2 * half, 3 - 2 * half) if step else ((1, 2) if half == 0 else (0, 1)):
-                        affine(blk, chunk)
-                if half == 0 and step + 1 < BLOCKS:
-                    deviation(step + 1)
+            if 0 < step:
+                if step + 1 < BLOCKS:
+                    for j in range(TILES):
+                        add_streams(step + 1, j)
+                deviation(step)
+            for pair in ((0, 1), (2, 3)):
+                if step + 3 < BLOCKS:
+                    for chunk in pair:
+                        affine(step + 3, chunk)
                 if step + 2 < BLOCKS:
-                    for j in (2 * half, 2 * half + 1):
+                    for j in pair:
                         turn_back(step + 2, j)
-            normalise(step)
+            take_off_means(step)
+            scale_and_store(step)

@@ -20,6 +20,10 @@ BLOCKS = L * B // (TILES * P)
 CHUNKS = D // P
 WORDS = D // 2
 LATE = (BLOCKS - 2, BLOCKS - 1)
+WARM = 8
+X_ON_TENSOR = range(6, BLOCKS)
+NORM_ON_GPSIMD = (0, 0, 0, 1, 1, 1, 1, 1)
+ON_VECTOR = range(4, 8)
 LAST = CHUNKS - 1
 ON_SCALAR = range(1, 5)
 KEEP = [blk for blk in range(BLOCKS) if blk not in ON_SCALAR]
@@ -159,16 +163,20 @@ def tile_coattention_pb_t_kernel(tc, x, res_a, ctx_v, W_v, bn_v_g, bn_v_b, prelu
                 )
 
             def multiply(blk):
-                if blk + 2 < BLOCKS:
-                    grouped[blk + 2] = turn_k_onto_partitions(ctx_sb[blk + 2])
-                if blk + 1 < BLOCKS:
-                    quantise(blk + 1)
                 for chunk in range(CHUNKS):
+                    if chunk == 1 and blk + 1 < BLOCKS:
+                        quantise(blk + 1)
                     if chunk % 2 == 0:
                         y_t = conv_pass(blk, chunk, y_psum, "y")
                     else:
                         y_t = conv_pass(blk, chunk, turn_psum, "turn")
                     take_statistics(blk, chunk, y_t)
+                if blk + 2 < BLOCKS:
+                    grouped[blk + 2] = turn_k_onto_partitions(ctx_sb[blk + 2])
+
+            warm_bank = turn_psum.tile([P, P], F32, name="warm_bank", tag="turn")
+            for again in range(WARM):
+                nc.tensor.matmul(out=warm_bank[:], lhsT=ident_f32[:], rhs=ident_f32[:], start=True, stop=True)
 
             w_grouped = turn_k_onto_partitions(w_sb, vector_helps=True)
             grouped[0] = turn_k_onto_partitions(ctx_sb[0], vector_helps=True)
@@ -188,6 +196,8 @@ def tile_coattention_pb_t_kernel(tc, x, res_a, ctx_v, W_v, bn_v_g, bn_v_b, prelu
             ln_both = gain_psum.tile([P, 2, D], BF16, name="ln_both")
             nc.tensor.matmul(out=ln_both[:, 0, :], lhsT=ones[:], rhs=ln_rows[:, 0, :], start=True, stop=True)
             nc.tensor.matmul(out=ln_both[:, 1, :], lhsT=ones[:], rhs=ln_rows[:, 1, :], start=True, stop=True)
+            ln_sb = const.tile([P, 2, D], BF16, name="ln_sb")
+            nc.scalar.copy(out=ln_sb[:].rearrange("p v d -> p (v d)"), in_=ln_both[:].rearrange("p v d -> p (v d)"))
             ln_gain = ln_both[:, 0, :]
             ln_bias = ln_both[:, 1, :]
             one_minus_slope = const.tile([P, 1], F32, name="one_minus_slope")
@@ -199,6 +209,8 @@ def tile_coattention_pb_t_kernel(tc, x, res_a, ctx_v, W_v, bn_v_g, bn_v_b, prelu
                 out=flip[:], in0=one_minus_slope[:], scalar1=0.0, scalar2=2.0, op0=ALU.is_ge, op1=ALU.mult
             )
             nc.gpsimd.tensor_scalar(out=flip[:], in0=flip[:], scalar1=1.0, scalar2=None, op0=ALU.subtract)
+            flip_ident = const.tile([P, P], BF16, name="flip_ident")
+            nc.gpsimd.tensor_scalar(out=flip_ident[:], in0=ident_bf[:], scalar1=flip[:], scalar2=0.0, op0=ALU.mult, op1=ALU.add)
             parts = const.tile([P, 6], F32, name="parts")
             nc.gpsimd.tensor_tensor(out=parts[:, 0:1], in0=flip[:], in1=slope_bf[:], op=ALU.mult)
             nc.gpsimd.tensor_tensor(out=parts[:, 1:2], in0=flip[:], in1=one_minus_slope[:], op=ALU.mult)
@@ -238,7 +250,7 @@ def tile_coattention_pb_t_kernel(tc, x, res_a, ctx_v, W_v, bn_v_g, bn_v_b, prelu
         sums = []
         for blk in range(BLOCKS):
             sum_t = sum_pool.tile([P, TILES, D], F32, name="sum_t%d" % blk)
-            for j in range(TILES):
+            for j in range(TILES if blk not in X_ON_TENSOR else 0):
                 nc.gpsimd.tensor_tensor(out=sum_t[:, j, :], in0=x_sb[blk][:, j, :], in1=res_sb[blk][:, j, :], op=ALU.add)
             sums.append(sum_t)
 
@@ -291,19 +303,24 @@ def tile_coattention_pb_t_kernel(tc, x, res_a, ctx_v, W_v, bn_v_g, bn_v_b, prelu
 
         def turn_back(blk, j):
             back = turn_psum.tile([P, D], F32, name="back", tag="turn")
+            with_x = blk in X_ON_TENSOR
+            if with_x:
+                nc.tensor.matmul(out=back[:], lhsT=flip_ident[:], rhs=x_sb[blk][:, j, :], start=True, stop=False)
             for chunk in range(CHUNKS):
                 for term, first in ((lines[(blk, chunk)], True), (relus[(blk, chunk)], False)):
                     nc.tensor.matmul(
                         out=back[:, chunk * P : (chunk + 1) * P], lhsT=term[:, j * P : (j + 1) * P],
-                        rhs=ident_f32[:], is_transpose=True, start=first, stop=not first,
+                        rhs=ident_f32[:], is_transpose=True, start=first and not with_x,
+                        stop=(not first) and (chunk == CHUNKS - 1 or not with_x),
                     )
             turned_back[(blk, j)] = back
 
         def add_streams(blk, j):
             if j == 0:
                 row_sums[blk] = small.tile([P, TILES], F32, name="row_sum")
+            rest = res_sb[blk] if blk in X_ON_TENSOR else sums[blk]
             nc.vector.scalar_tensor_tensor(
-                out=sums[blk][:, j, :], in0=turned_back[(blk, j)][:], scalar=flip[:], in1=sums[blk][:, j, :],
+                out=sums[blk][:, j, :], in0=turned_back[(blk, j)][:], scalar=flip[:], in1=rest[:, j, :],
                 op0=ALU.mult, op1=ALU.add, accum_out=row_sums[blk][:, j : j + 1],
             )
 
@@ -325,21 +342,35 @@ def tile_coattention_pb_t_kernel(tc, x, res_a, ctx_v, W_v, bn_v_g, bn_v_b, prelu
             row_rstds[blk] = row_rstd
 
         def take_off_means(blk):
-            for j in range(TILES):
+            for j in range(NORM_ON_GPSIMD[blk], TILES):
                 nc.vector.scalar_tensor_tensor(
                     out=sums[blk][:, j, :], in0=sums[blk][:, j, :], scalar=neg_means[blk][:, j : j + 1], in1=ln_gain,
                     op0=ALU.add, op1=ALU.mult,
                 )
 
-        def scale_and_store(blk):
+        def store(blk, j):
             l_rows, b_rows = block_rows(blk)
             first_b = (blk % (B // TILES)) * TILES
-            for j in range(TILES):
+            nc.sync.dma_start(out=out[l_rows, first_b + j : first_b + j + 1, :], in_=sums[blk][:, j : j + 1, :])
+
+        def scale_and_store(blk):
+            for j in range(NORM_ON_GPSIMD[blk], TILES):
                 nc.vector.scalar_tensor_tensor(
                     out=sums[blk][:, j, :], in0=sums[blk][:, j, :], scalar=row_rstds[blk][:, j : j + 1], in1=ln_bias,
                     op0=ALU.mult, op1=ALU.add,
                 )
-                nc.sync.dma_start(out=out[l_rows, first_b + j : first_b + j + 1, :], in_=sums[blk][:, j : j + 1, :])
+                store(blk, j)
+
+        def normalise_on_gpsimd(blk):
+            for j in range(NORM_ON_GPSIMD[blk]):
+                row_tile = sums[blk][:, j, :]
+                nc.gpsimd.tensor_scalar(
+                    out=row_tile, in0=row_tile, scalar1=neg_means[blk][:, j : j + 1], scalar2=row_rstds[blk][:, j : j + 1],
+                    op0=ALU.add, op1=ALU.mult,
+                )
+                nc.gpsimd.tensor_tensor(out=row_tile, in0=row_tile, in1=ln_sb[:, 0, :], op=ALU.mult)
+                nc.gpsimd.tensor_tensor(out=row_tile, in0=row_tile, in1=ln_sb[:, 1, :], op=ALU.add)
+                store(blk, j)
 
         for chunk in range(CHUNKS):
             for blk in LATE:
@@ -372,17 +403,23 @@ def tile_coattention_pb_t_kernel(tc, x, res_a, ctx_v, W_v, bn_v_g, bn_v_b, prelu
         affine(2, 2)
 
         for step in range(BLOCKS):
+            nxt = step + 3
+            shared = nxt in ON_VECTOR
             if 0 < step:
                 if step + 1 < BLOCKS:
                     for j in range(TILES):
                         add_streams(step + 1, j)
                 deviation(step)
-            for pair in ((0, 1), (2, 3)):
-                if step + 3 < BLOCKS:
+            if shared:
+                affine(nxt, LAST, on_vector=True)
+            take_off_means(step)
+            scale_and_store(step)
+            normalise_on_gpsimd(step)
+            for pair in ((0, 1), (2, LAST)):
+                if nxt < BLOCKS:
                     for chunk in pair:
-                        affine(step + 3, chunk)
+                        if (nxt, chunk) not in lines:
+                            affine(nxt, chunk)
                 if step + 2 < BLOCKS:
                     for j in pair:
                         turn_back(step + 2, j)
-            take_off_means(step)
-            scale_and_store(step)

@@ -20,10 +20,10 @@ BLOCKS = L * B // (TILES * P)
 CHUNKS = D // P
 WORDS = D // 2
 LATE = (BLOCKS - 2, BLOCKS - 1)
-WARM = 8
-X_ON_TENSOR = range(6, BLOCKS)
-NORM_ON_GPSIMD = (0, 0, 0, 1, 1, 1, 1, 1)
-ON_VECTOR = range(4, 8)
+WARM = 6
+X_ON_TENSOR = ()
+NORM_ON_GPSIMD = (0, 0, 0, 0, 0, 1, 1, 1)
+ON_VECTOR = (4, 5)
 LAST = CHUNKS - 1
 ON_SCALAR = range(1, 5)
 KEEP = [blk for blk in range(BLOCKS) if blk not in ON_SCALAR]
@@ -44,9 +44,8 @@ def tile_coattention_pb_t_kernel(tc, x, res_a, ctx_v, W_v, bn_v_g, bn_v_b, prelu
         y_psum = stack.enter_context(tc.psum_pool(name="y_psum", bufs=3))
         turn_psum = stack.enter_context(tc.psum_pool(name="turn_psum", bufs=4))
 
-        def block_rows(blk):
-            group, half = divmod(blk, B // TILES)
-            return slice(group * P, (group + 1) * P), slice(half * TILES, (half + 1) * TILES)
+        def by_partition(rows):
+            return rows.rearrange("(p j) d -> p j d", j=TILES)
 
         eps_bn = const.tile([P, 1], F32, name="eps_bn")
         nc.vector.memset(eps_bn[:], EPS_BN)
@@ -74,25 +73,24 @@ def tile_coattention_pb_t_kernel(tc, x, res_a, ctx_v, W_v, bn_v_g, bn_v_b, prelu
 
         with tc.tile_pool(name="ctx", bufs=4) as ctx_pool, tc.tile_pool(name="stage", bufs=3) as stage:
             w_sb = keep.tile([P, CHUNKS * D], BF16, name="w_sb")
-            nc.sync.dma_start(
-                out=w_sb[:].rearrange("p (c k) -> p c k", c=CHUNKS), in_=W_v.rearrange("(c p) k -> p c k", p=P)
-            )
+            def load_rows(rows_sb, source, parts):
+                rows = rows_sb[:].rearrange("p (t k) -> p t k", t=TILES)
+                for part in range(parts):
+                    tiles = slice(part * TILES // parts, (part + 1) * TILES // parts)
+                    nc.sync.dma_start(out=rows[:, tiles, :], in_=source[:, tiles, :])
+
+            load_rows(w_sb, W_v.rearrange("(c p) k -> p c k", p=P), 2)
             ctx_sb = []
             for blk in range(BLOCKS):
-                l_rows, b_rows = block_rows(blk)
                 ctx_t = ctx_pool.tile([P, TILES * D], BF16, name="ctx_t")
-                nc.sync.dma_start(
-                    out=ctx_t[:].rearrange("p (b k) -> p b k", b=TILES),
-                    in_=ctx_v[b_rows, l_rows, :].rearrange("b l k -> l b k"),
-                )
+                load_rows(ctx_t, by_partition(ctx_v[blk, :, :]), 2 if blk == 0 else 1)
                 ctx_sb.append(ctx_t)
             x_sb, res_sb = [], []
             for blk in range(BLOCKS):
-                l_rows, b_rows = block_rows(blk)
                 x_t = keep.tile([P, TILES, D], BF16, name="x_t%d" % blk)
-                nc.sync.dma_start(out=x_t[:], in_=x[l_rows, b_rows, :])
+                nc.sync.dma_start(out=x_t[:], in_=by_partition(x[:, blk, :]))
                 res_t = keep.tile([P, TILES, D], BF16, name="res_t%d" % blk)
-                nc.sync.dma_start(out=res_t[:], in_=res_a[b_rows, l_rows, :].rearrange("b l d -> l b d"))
+                nc.sync.dma_start(out=res_t[:], in_=by_partition(res_a[blk, :, :]))
                 x_sb.append(x_t)
                 res_sb.append(res_t)
 
@@ -267,10 +265,12 @@ def tile_coattention_pb_t_kernel(tc, x, res_a, ctx_v, W_v, bn_v_g, bn_v_b, prelu
                 bias=eps_bn[:], scale=1.0,
             )
 
-        def prepare(chunk):
+        def make_scales(chunk):
             nc.vector.tensor_scalar_mul(
                 out=scales[:, chunk, :], in0=factors[:, chunk, :], scalar1=bn_rstd[:, chunk : chunk + 1]
             )
+
+        def make_shifts(chunk):
             nc.vector.scalar_tensor_tensor(
                 out=shifts[:, chunk, :], in0=scales[:, chunk, 2:6], scalar=mean_var[:, chunk, 0:1],
                 in1=constants[:, chunk, :], op0=ALU.mult, op1=ALU.add,
@@ -302,18 +302,23 @@ def tile_coattention_pb_t_kernel(tc, x, res_a, ctx_v, W_v, bn_v_g, bn_v_b, prelu
             relus[(blk, chunk)] = relu
 
         def turn_back(blk, j):
-            back = turn_psum.tile([P, D], F32, name="back", tag="turn")
-            with_x = blk in X_ON_TENSOR
-            if with_x:
-                nc.tensor.matmul(out=back[:], lhsT=flip_ident[:], rhs=x_sb[blk][:, j, :], start=True, stop=False)
             for chunk in range(CHUNKS):
-                for term, first in ((lines[(blk, chunk)], True), (relus[(blk, chunk)], False)):
+                turn_chunk_back(blk, j, chunk)
+
+        def turn_chunk_back(blk, j, chunk):
+            with_x = blk in X_ON_TENSOR
+            if (blk, j) not in turned_back:
+                turned_back[(blk, j)] = turn_psum.tile([P, D], F32, name="back", tag="turn")
+                if with_x:
                     nc.tensor.matmul(
-                        out=back[:, chunk * P : (chunk + 1) * P], lhsT=term[:, j * P : (j + 1) * P],
-                        rhs=ident_f32[:], is_transpose=True, start=first and not with_x,
-                        stop=(not first) and (chunk == CHUNKS - 1 or not with_x),
+                        out=turned_back[(blk, j)][:], lhsT=flip_ident[:], rhs=x_sb[blk][:, j, :], start=True, stop=False
                     )
-            turned_back[(blk, j)] = back
+            for term, first in ((lines[(blk, chunk)], True), (relus[(blk, chunk)], False)):
+                nc.tensor.matmul(
+                    out=turned_back[(blk, j)][:, chunk * P : (chunk + 1) * P], lhsT=term[:, j * P : (j + 1) * P],
+                    rhs=ident_f32[:], is_transpose=True, start=first and not with_x,
+                    stop=(not first) and (chunk == CHUNKS - 1 or not with_x),
+                )
 
         def add_streams(blk, j):
             if j == 0:
@@ -349,9 +354,7 @@ def tile_coattention_pb_t_kernel(tc, x, res_a, ctx_v, W_v, bn_v_g, bn_v_b, prelu
                 )
 
         def store(blk, j):
-            l_rows, b_rows = block_rows(blk)
-            first_b = (blk % (B // TILES)) * TILES
-            nc.sync.dma_start(out=out[l_rows, first_b + j : first_b + j + 1, :], in_=sums[blk][:, j : j + 1, :])
+            nc.sync.dma_start(out=by_partition(out[:, blk, :])[:, j : j + 1, :], in_=sums[blk][:, j : j + 1, :])
 
         def scale_and_store(blk):
             for j in range(NORM_ON_GPSIMD[blk], TILES):
@@ -372,35 +375,58 @@ def tile_coattention_pb_t_kernel(tc, x, res_a, ctx_v, W_v, bn_v_g, bn_v_b, prelu
                 nc.gpsimd.tensor_tensor(out=row_tile, in0=row_tile, in1=ln_sb[:, 1, :], op=ALU.add)
                 store(blk, j)
 
-        for chunk in range(CHUNKS):
-            for blk in LATE:
-                take_statistics(blk, chunk, conv_pass(blk, chunk, turn_psum, "turn"))
-            if 0 < chunk:
-                prepare(chunk - 1)
-            aggregate(chunk)
-            if 0 < chunk:
-                affine(0, chunk - 1)
-        prepare(LAST)
-        affine(0, LAST, on_vector=True)
-        affine(1, LAST, on_vector=True)
+        first_late, second_late = LATE
+
+        def late_statistics(blk, chunk):
+            take_statistics(blk, chunk, conv_pass(blk, chunk, turn_psum, "turn"))
+
+        def turn_block_0(chunk):
+            for j in range(TILES):
+                turn_chunk_back(0, j, chunk)
+
+        late_statistics(first_late, 0)
+        late_statistics(second_late, 0)
+        late_statistics(first_late, 1)
+        aggregate(0)
+        late_statistics(second_late, 1)
+        make_scales(0)
+        late_statistics(first_late, 2)
+        make_shifts(0)
+        aggregate(1)
+        affine(0, 0)
+        late_statistics(second_late, 2)
+        make_scales(1)
+        late_statistics(first_late, LAST)
+        make_shifts(1)
+        aggregate(2)
+        affine(0, 1)
+        late_statistics(second_late, LAST)
+        make_scales(2)
+        turn_block_0(0)
+        make_shifts(2)
+        aggregate(LAST)
+        affine(0, 2, on_vector=True)
         affine(1, 0)
+        turn_block_0(1)
+        make_scales(LAST)
+        make_shifts(LAST)
+        affine(0, LAST, on_vector=True)
+        turn_block_0(2)
+        affine(1, LAST, on_vector=True)
         affine(1, 1)
-        for half in range(2):
-            for j in (2 * half, 2 * half + 1):
-                turn_back(0, j)
-            if half == 0:
-                affine(1, 2)
+        turn_block_0(LAST)
+        affine(1, 2)
         for j in range(TILES):
             add_streams(0, j)
         deviation(0)
         affine(2, LAST, on_vector=True)
-        affine(2, 0)
+        affine(2, 2, on_vector=True)
         for j in range(TILES):
             turn_back(1, j)
+        affine(2, 0)
         affine(2, 1)
         for j in range(TILES):
             add_streams(1, j)
-        affine(2, 2)
 
         for step in range(BLOCKS):
             nxt = step + 3

@@ -22,8 +22,9 @@ WORDS = D // 2
 LATE = (BLOCKS - 2, BLOCKS - 1)
 WARM = 6
 X_ON_TENSOR = ()
-NORM_ON_GPSIMD = (0, 0, 0, 0, 0, 1, 1, 1)
-ON_VECTOR = (4, 5)
+NORM_ON_GPSIMD = (0, 0, 0, 1, 1, 1, 2, 1)
+N_ON_SCALAR = (6, 7)
+ON_VECTOR = (4,)
 LAST = CHUNKS - 1
 ON_SCALAR = range(1, 5)
 KEEP = [blk for blk in range(BLOCKS) if blk not in ON_SCALAR]
@@ -194,7 +195,7 @@ def tile_coattention_pb_t_kernel(tc, x, res_a, ctx_v, W_v, bn_v_g, bn_v_b, prelu
             ln_both = gain_psum.tile([P, 2, D], BF16, name="ln_both")
             nc.tensor.matmul(out=ln_both[:, 0, :], lhsT=ones[:], rhs=ln_rows[:, 0, :], start=True, stop=True)
             nc.tensor.matmul(out=ln_both[:, 1, :], lhsT=ones[:], rhs=ln_rows[:, 1, :], start=True, stop=True)
-            ln_sb = const.tile([P, 2, D], BF16, name="ln_sb")
+            ln_sb = const.tile([P, 2, D], F32, name="ln_sb")
             nc.scalar.copy(out=ln_sb[:].rearrange("p v d -> p (v d)"), in_=ln_both[:].rearrange("p v d -> p (v d)"))
             ln_gain = ln_both[:, 0, :]
             ln_bias = ln_both[:, 1, :]
@@ -367,10 +368,19 @@ def tile_coattention_pb_t_kernel(tc, x, res_a, ctx_v, W_v, bn_v_g, bn_v_b, prelu
         def normalise_on_gpsimd(blk):
             for j in range(NORM_ON_GPSIMD[blk]):
                 row_tile = sums[blk][:, j, :]
-                nc.gpsimd.tensor_scalar(
-                    out=row_tile, in0=row_tile, scalar1=neg_means[blk][:, j : j + 1], scalar2=row_rstds[blk][:, j : j + 1],
-                    op0=ALU.add, op1=ALU.mult,
-                )
+                rstd = row_rstds[blk][:, j : j + 1]
+                if blk not in N_ON_SCALAR:
+                    nc.gpsimd.tensor_scalar(
+                        out=row_tile, in0=row_tile, scalar1=neg_means[blk][:, j : j + 1], scalar2=rstd,
+                        op0=ALU.add, op1=ALU.mult,
+                    )
+                    nc.gpsimd.tensor_tensor(out=row_tile, in0=row_tile, in1=ln_sb[:, 0, :], op=ALU.mult)
+                    nc.gpsimd.tensor_tensor(out=row_tile, in0=row_tile, in1=ln_sb[:, 1, :], op=ALU.add)
+                    store(blk, j)
+                    continue
+                offset = small.tile([P, 1], F32, name="offset%d" % j)
+                nc.scalar.activation(out=offset[:], in_=neg_means[blk][:, j : j + 1], func=ACT.Copy, scale=rstd)
+                nc.scalar.activation(out=row_tile, in_=row_tile, func=ACT.Identity, scale=rstd, bias=offset[:])
                 nc.gpsimd.tensor_tensor(out=row_tile, in0=row_tile, in1=ln_sb[:, 0, :], op=ALU.mult)
                 nc.gpsimd.tensor_tensor(out=row_tile, in0=row_tile, in1=ln_sb[:, 1, :], op=ALU.add)
                 store(blk, j)
@@ -436,11 +446,11 @@ def tile_coattention_pb_t_kernel(tc, x, res_a, ctx_v, W_v, bn_v_g, bn_v_b, prelu
                     for j in range(TILES):
                         add_streams(step + 1, j)
                 deviation(step)
+            normalise_on_gpsimd(step)
             if shared:
                 affine(nxt, LAST, on_vector=True)
             take_off_means(step)
             scale_and_store(step)
-            normalise_on_gpsimd(step)
             for pair in ((0, 1), (2, LAST)):
                 if nxt < BLOCKS:
                     for chunk in pair:

@@ -22,9 +22,9 @@ WORDS = D // 2
 LATE = (BLOCKS - 2, BLOCKS - 1)
 WARM = 6
 X_ON_TENSOR = ()
-NORM_ON_GPSIMD = (0, 0, 0, 1, 1, 1, 2, 1)
-N_ON_SCALAR = (6, 7)
-ON_VECTOR = (4,)
+NORM_ON_GPSIMD = (0, 0, 0, 0, 1, 1, 1, 0)
+N_ON_SCALAR = ()
+ON_VECTOR = (4, 5)
 LAST = CHUNKS - 1
 ON_SCALAR = range(1, 5)
 KEEP = [blk for blk in range(BLOCKS) if blk not in ON_SCALAR]
@@ -376,14 +376,12 @@ def tile_coattention_pb_t_kernel(tc, x, res_a, ctx_v, W_v, bn_v_g, bn_v_b, prelu
                     )
                     nc.gpsimd.tensor_tensor(out=row_tile, in0=row_tile, in1=ln_sb[:, 0, :], op=ALU.mult)
                     nc.gpsimd.tensor_tensor(out=row_tile, in0=row_tile, in1=ln_sb[:, 1, :], op=ALU.add)
-                    store(blk, j)
                     continue
                 offset = small.tile([P, 1], F32, name="offset%d" % j)
                 nc.scalar.activation(out=offset[:], in_=neg_means[blk][:, j : j + 1], func=ACT.Copy, scale=rstd)
                 nc.scalar.activation(out=row_tile, in_=row_tile, func=ACT.Identity, scale=rstd, bias=offset[:])
                 nc.gpsimd.tensor_tensor(out=row_tile, in0=row_tile, in1=ln_sb[:, 0, :], op=ALU.mult)
                 nc.gpsimd.tensor_tensor(out=row_tile, in0=row_tile, in1=ln_sb[:, 1, :], op=ALU.add)
-                store(blk, j)
 
         first_late, second_late = LATE
 
@@ -451,6 +449,8 @@ def tile_coattention_pb_t_kernel(tc, x, res_a, ctx_v, W_v, bn_v_g, bn_v_b, prelu
                 affine(nxt, LAST, on_vector=True)
             take_off_means(step)
             scale_and_store(step)
+            for j in range(NORM_ON_GPSIMD[step]):
+                store(step, j)
             for pair in ((0, 1), (2, LAST)):
                 if nxt < BLOCKS:
                     for chunk in pair:

from contextlib import ExitStack

import concourse.mybir as mybir
from concourse.masks import make_identity

F32 = mybir.dt.float32
BF16 = mybir.dt.bfloat16
U32 = mybir.dt.uint32
U8 = mybir.dt.uint8
FP8X4 = mybir.dt.float8_e4m3fn_x4
ALU = mybir.AluOpType
ACT = mybir.ActivationFunctionType

L, B, D = 512, 8, 512
P = 128
EPS_BN = 1e-5
EPS_LN = 1e-5
TILES = 4
BLOCKS = L * B // (TILES * P)
CHUNKS = D // P
WORDS = D // 2
LATE = (BLOCKS - 2, BLOCKS - 1)
WARM = 6
X_ON_TENSOR = ()
NORM_ON_GPSIMD = (0, 0, 0, 0, 1, 1, 1, 0)
N_ON_SCALAR = ()
ON_VECTOR = (4, 5)
LAST = CHUNKS - 1
ON_SCALAR = range(1, 5)
KEEP = [blk for blk in range(BLOCKS) if blk not in ON_SCALAR]
REPEAT = 2
FLOPS = 2 * L * B * D * D


def tile_coattention_pb_t_kernel(tc, x, res_a, ctx_v, W_v, bn_v_g, bn_v_b, prelu_v, ln_g, ln_b, out):
    nc = tc.nc
    with ExitStack() as stack:
        stack.enter_context(tc.manual_schedule())
        const = stack.enter_context(tc.tile_pool(name="const", bufs=1))
        keep = stack.enter_context(tc.tile_pool(name="keep", bufs=1))
        branch = stack.enter_context(tc.tile_pool(name="branch", bufs=4))
        scrap = stack.enter_context(tc.tile_pool(name="scrap", bufs=4))
        small = stack.enter_context(tc.tile_pool(name="small", bufs=3))
        gain_psum = stack.enter_context(tc.psum_pool(name="gain_psum", bufs=1))
        y_psum = stack.enter_context(tc.psum_pool(name="y_psum", bufs=3))
        turn_psum = stack.enter_context(tc.psum_pool(name="turn_psum", bufs=4))

        def by_partition(rows):
            return rows.rearrange("(p j) d -> p j d", j=TILES)

        eps_bn = const.tile([P, 1], F32, name="eps_bn")
        nc.vector.memset(eps_bn[:], EPS_BN)
        eps_ln = const.tile([P, 1], F32, name="eps_ln")
        nc.vector.memset(eps_ln[:], EPS_LN)
        warm = const.tile([P, 1], F32, name="warm")
        nc.scalar.activation(out=warm[:], in_=eps_bn[:], func=ACT.Abs_reciprocal_sqrt)

        ones = const.tile([P, P], BF16, name="ones")
        nc.vector.memset(ones[:], 1.0)
        bn_rows = const.tile([P, P], BF16, name="bn_rows")
        nc.vector.memset(bn_rows[:], 0.0)
        ln_rows = const.tile([P, 2, D], BF16, name="ln_rows")
        nc.vector.memset(ln_rows[:], 0.0)
        slope_bf = const.tile([P, 1], BF16, name="slope_bf")
        nc.scalar.dma_start(out=bn_rows[0:CHUNKS, :], in_=bn_v_g.rearrange("(c p) -> c p", p=P))
        nc.scalar.dma_start(out=bn_rows[CHUNKS : 2 * CHUNKS, :], in_=bn_v_b.rearrange("(c p) -> c p", p=P))
        nc.scalar.dma_start(out=ln_rows[0:1, 0, :], in_=ln_g.rearrange("(o d) -> o d", o=1))
        nc.scalar.dma_start(out=ln_rows[0:1, 1, :], in_=ln_b.rearrange("(o d) -> o d", o=1))
        nc.scalar.dma_start(out=slope_bf[:], in_=prelu_v.partition_broadcast(P))
        ident_f32 = const.tile([P, P], F32, name="ident_f32")
        make_identity(nc, ident_f32[:])
        ident_bf = const.tile([P, P], BF16, name="ident_bf")
        make_identity(nc, ident_bf[:])

        with tc.tile_pool(name="ctx", bufs=4) as ctx_pool, tc.tile_pool(name="stage", bufs=3) as stage:
            w_sb = keep.tile([P, CHUNKS * D], BF16, name="w_sb")
            def load_rows(rows_sb, source, parts):
                rows = rows_sb[:].rearrange("p (t k) -> p t k", t=TILES)
                for part in range(parts):
                    tiles = slice(part * TILES // parts, (part + 1) * TILES // parts)
                    nc.sync.dma_start(out=rows[:, tiles, :], in_=source[:, tiles, :])

            load_rows(w_sb, W_v.rearrange("(c p) k -> p c k", p=P), 2)
            ctx_sb = []
            for blk in range(BLOCKS):
                ctx_t = ctx_pool.tile([P, TILES * D], BF16, name="ctx_t")
                load_rows(ctx_t, by_partition(ctx_v[blk, :, :]), 2 if blk == 0 else 1)
                ctx_sb.append(ctx_t)
            x_sb, res_sb = [], []
            for blk in range(BLOCKS):
                x_t = keep.tile([P, TILES, D], BF16, name="x_t%d" % blk)
                nc.sync.dma_start(out=x_t[:], in_=by_partition(x[:, blk, :]))
                res_t = keep.tile([P, TILES, D], BF16, name="res_t%d" % blk)
                nc.sync.dma_start(out=res_t[:], in_=by_partition(res_a[blk, :, :]))
                x_sb.append(x_t)
                res_sb.append(res_t)

            w_codes = keep.tile([P, D], U32, name="w_codes", align_bytes=64)
            w_scales = keep.tile([P, D], U8, name="w_scales", align_bytes=64)
            ctx_codes = keep.tile([P, BLOCKS, TILES * P], U32, name="ctx_codes", align_bytes=64)
            ctx_scales = keep.tile([P, BLOCKS, TILES * P], U8, name="ctx_scales", align_bytes=64)

            def turn_k_onto_partitions(rows_sb, vector_helps=False):
                words = rows_sb[:].bitcast(F32)
                grouped = stage.tile([P, TILES * P * 4], BF16, name="grouped", align_bytes=64)
                grouped_words = grouped[:].bitcast(F32).rearrange("p (c u) -> p c u", u=2)
                for pair in range(TILES // 2):
                    turned = turn_psum.tile([P, 2, 2 * P], F32, name="turned", tag="turn")
                    for i in range(2):
                        for u in range(2):
                            row_words = (2 * pair + i) * WORDS
                            nc.tensor.transpose(
                                out=turned[:, u, i * P : (i + 1) * P], in_=words[:, row_words + u : row_words + WORDS : 2], identity=ident_f32[:]
                            )
                    copied = grouped_words[:, 2 * pair * P : 2 * (pair + 1) * P, :]
                    if vector_helps and pair == 1:
                        nc.vector.tensor_copy(out=copied, in_=turned[:].rearrange("p u r -> p r u"))
                    else:
                        nc.scalar.copy(out=copied, in_=turned[:].rearrange("p u r -> p r u"))
                return grouped

            def conv_pass(blk, chunk, bank_pool, bank_tag, repeat=1):
                y_t = bank_pool.tile([P, TILES * P], F32, name="y_t", tag=bank_tag)
                c_cols = slice(chunk * P, (chunk + 1) * P)
                for again in range(repeat):
                    nc.tensor.matmul_mx(
                        out=y_t[:],
                        lhsT=w_codes[:, c_cols].bitcast(FP8X4),
                        lhsT_scale=w_scales[:, c_cols],
                        rhs=ctx_codes[:, blk, :].bitcast(FP8X4),
                        rhs_scale=ctx_scales[:, blk, :],
                        start=True,
                        stop=True,
                    )
                return y_t

            grouped = {}
            stats = keep.tile([P, CHUNKS, BLOCKS * 6], F32, name="stats")
            pivot_sums = keep.tile([P, 2, len(ON_SCALAR)], F32, name="pivot_sums")
            neg_pivot = keep.tile([P, 1], F32, name="neg_pivot")

            def take_statistics(blk, chunk, y_t):
                if chunk < LAST:
                    nc.vector.bn_stats(out=stats[:, chunk, blk * 6 : (blk + 1) * 6], in_=y_t[:])
                elif blk in ON_SCALAR:
                    if blk == ON_SCALAR[0]:
                        nc.scalar.mul(out=neg_pivot[:], in_=stats[:, LAST, 1:2], mul=-1.0)
                    for power, func in enumerate((ACT.Identity, ACT.Square)):
                        unread = scrap.tile([P, D], BF16, name="unread")
                        column = ON_SCALAR.index(blk)
                        nc.scalar.activation(
                            out=unread[:], in_=y_t[:], func=func, bias=neg_pivot[:], scale=1.0,
                            accum_out=pivot_sums[:, power, column : column + 1],
                        )
                else:
                    place = KEEP.index(blk)
                    nc.vector.bn_stats(out=stats[:, chunk, place * 6 : (place + 1) * 6], in_=y_t[:])

            def quantise(blk):
                nc.vector.quantize_mx(
                    out=ctx_codes[:, blk, :].bitcast(FP8X4), scales=ctx_scales[:, blk, :], in_=grouped[blk][:]
                )

            def multiply(blk):
                for chunk in range(CHUNKS):
                    if chunk == 1 and blk + 1 < BLOCKS:
                        quantise(blk + 1)
                    if chunk % 2 == 0:
                        y_t = conv_pass(blk, chunk, y_psum, "y")
                    else:
                        y_t = conv_pass(blk, chunk, turn_psum, "turn")
                    take_statistics(blk, chunk, y_t)
                if blk + 2 < BLOCKS:
                    grouped[blk + 2] = turn_k_onto_partitions(ctx_sb[blk + 2])

            warm_bank = turn_psum.tile([P, P], F32, name="warm_bank", tag="turn")
            for again in range(WARM):
                nc.tensor.matmul(out=warm_bank[:], lhsT=ident_f32[:], rhs=ident_f32[:], start=True, stop=True)

            w_grouped = turn_k_onto_partitions(w_sb, vector_helps=True)
            grouped[0] = turn_k_onto_partitions(ctx_sb[0], vector_helps=True)
            nc.vector.quantize_mx(out=w_codes[:].bitcast(FP8X4), scales=w_scales[:], in_=w_grouped[:])
            grouped[1] = turn_k_onto_partitions(ctx_sb[1])
            quantise(0)
            multiply(0)

            for blk in range(1, LATE[0]):
                multiply(blk)
            quantise(LATE[1])

            bn_turned = turn_psum.tile([P, P], BF16, name="bn_turned", tag="turn")
            nc.tensor.transpose(out=bn_turned[:], in_=bn_rows[:], identity=ident_bf[:])
            bn_cols = const.tile([P, 2 * CHUNKS], F32, name="bn_cols")
            nc.scalar.copy(out=bn_cols[:], in_=bn_turned[:, 0 : 2 * CHUNKS])
            ln_both = gain_psum.tile([P, 2, D], BF16, name="ln_both")
            nc.tensor.matmul(out=ln_both[:, 0, :], lhsT=ones[:], rhs=ln_rows[:, 0, :], start=True, stop=True)
            nc.tensor.matmul(out=ln_both[:, 1, :], lhsT=ones[:], rhs=ln_rows[:, 1, :], start=True, stop=True)
            ln_sb = const.tile([P, 2, D], F32, name="ln_sb")
            nc.scalar.copy(out=ln_sb[:].rearrange("p v d -> p (v d)"), in_=ln_both[:].rearrange("p v d -> p (v d)"))
            ln_gain = ln_both[:, 0, :]
            ln_bias = ln_both[:, 1, :]
            one_minus_slope = const.tile([P, 1], F32, name="one_minus_slope")
            nc.gpsimd.tensor_scalar(
                out=one_minus_slope[:], in0=slope_bf[:], scalar1=-1.0, scalar2=1.0, op0=ALU.mult, op1=ALU.add
            )
            flip = const.tile([P, 1], F32, name="flip")
            nc.gpsimd.tensor_scalar(
                out=flip[:], in0=one_minus_slope[:], scalar1=0.0, scalar2=2.0, op0=ALU.is_ge, op1=ALU.mult
            )
            nc.gpsimd.tensor_scalar(out=flip[:], in0=flip[:], scalar1=1.0, scalar2=None, op0=ALU.subtract)
            flip_ident = const.tile([P, P], BF16, name="flip_ident")
            nc.gpsimd.tensor_scalar(out=flip_ident[:], in0=ident_bf[:], scalar1=flip[:], scalar2=0.0, op0=ALU.mult, op1=ALU.add)
            parts = const.tile([P, 6], F32, name="parts")
            nc.gpsimd.tensor_tensor(out=parts[:, 0:1], in0=flip[:], in1=slope_bf[:], op=ALU.mult)
            nc.gpsimd.tensor_tensor(out=parts[:, 1:2], in0=flip[:], in1=one_minus_slope[:], op=ALU.mult)
            nc.gpsimd.tensor_scalar(out=parts[:, 2:4], in0=parts[:, 0:2], scalar1=-1.0, scalar2=None, op0=ALU.mult)
            nc.gpsimd.tensor_copy(out=parts[:, 4:5], in_=parts[:, 1:2])
            nc.gpsimd.tensor_scalar(out=parts[:, 5:6], in0=flip[:], scalar1=-1.0, scalar2=None, op0=ALU.mult)
            minus_parts = const.tile([P, 4], F32, name="minus_parts")
            nc.gpsimd.tensor_scalar(out=minus_parts[:], in0=parts[:, 2:6], scalar1=-1.0, scalar2=None, op0=ALU.mult)
            factors = const.tile([P, CHUNKS, 6], F32, name="factors")
            constants = const.tile([P, CHUNKS, 4], F32, name="constants")
            for chunk in range(CHUNKS):
                gamma = bn_cols[:, chunk : chunk + 1]
                beta = bn_cols[:, CHUNKS + chunk : CHUNKS + chunk + 1]
                nc.scalar.activation(out=factors[:, chunk, :], in_=parts[:], func=ACT.Copy, scale=gamma)
                nc.scalar.activation(out=constants[:, chunk, :], in_=minus_parts[:], func=ACT.Copy, scale=beta)

            count = len(ON_SCALAR) * TILES * P
            triple = stats[:, LAST, len(KEEP) * 6 : len(KEEP) * 6 + 3]
            nc.gpsimd.memset(triple[:, 0:1], float(count))
            totals = const.tile([P, 2], F32, name="totals")
            for power in range(2):
                unread_sums = const.tile([P, len(ON_SCALAR)], F32, name="unread_sums%d" % power)
                nc.scalar.activation(
                    out=unread_sums[:], in_=pivot_sums[:, power, :], func=ACT.Identity, scale=1.0,
                    accum_out=totals[:, power : power + 1],
                )
            neg_offset = const.tile([P, 1], F32, name="neg_offset")
            nc.scalar.mul(out=neg_offset[:], in_=totals[:, 0:1], mul=-1.0 / count)
            nc.scalar.activation(
                out=triple[:, 1:2], in_=neg_offset[:], func=ACT.Identity, scale=-1.0, bias=stats[:, LAST, 1:2]
            )
            nc.scalar.activation(
                out=triple[:, 2:3], in_=totals[:, 0:1], func=ACT.Identity, scale=neg_offset[:], bias=totals[:, 1:2]
            )

        sum_pool = stack.enter_context(tc.tile_pool(name="sums", bufs=1))
        sums = []
        for blk in range(BLOCKS):
            sum_t = sum_pool.tile([P, TILES, D], F32, name="sum_t%d" % blk)
            for j in range(TILES if blk not in X_ON_TENSOR else 0):
                nc.gpsimd.tensor_tensor(out=sum_t[:, j, :], in0=x_sb[blk][:, j, :], in1=res_sb[blk][:, j, :], op=ALU.add)
            sums.append(sum_t)

        mean_var = const.tile([P, CHUNKS, 2], F32, name="mean_var")
        bn_rstd = const.tile([P, CHUNKS], F32, name="bn_rstd")
        scales = const.tile([P, CHUNKS, 6], F32, name="scales")
        shifts = const.tile([P, CHUNKS, 4], F32, name="shifts")

        def aggregate(chunk):
            values = len(KEEP) * 6 + 3 if chunk == LAST else BLOCKS * 6
            nc.vector.bn_aggr(out=mean_var[:, chunk, :], in_=stats[:, chunk, 0:values])
            nc.scalar.activation(
                out=bn_rstd[:, chunk : chunk + 1], in_=mean_var[:, chunk, 1:2], func=ACT.Abs_reciprocal_sqrt,
                bias=eps_bn[:], scale=1.0,
            )

        def make_scales(chunk):
            nc.vector.tensor_scalar_mul(
                out=scales[:, chunk, :], in0=factors[:, chunk, :], scalar1=bn_rstd[:, chunk : chunk + 1]
            )

        def make_shifts(chunk):
            nc.vector.scalar_tensor_tensor(
                out=shifts[:, chunk, :], in0=scales[:, chunk, 2:6], scalar=mean_var[:, chunk, 0:1],
                in1=constants[:, chunk, :], op0=ALU.mult, op1=ALU.add,
            )

        lines, relus, turned_back, row_sums, neg_means, row_rstds = {}, {}, {}, {}, {}, {}

        def affine(blk, chunk, on_vector=False):
            y_t = conv_pass(blk, chunk, y_psum, "y", REPEAT)
            line = branch.tile([P, TILES * P], F32, name="line%d" % chunk)
            relu = branch.tile([P, TILES * P], F32, name="relu%d" % chunk)
            line_scale = scales[:, chunk, 0:1]
            relu_scale = scales[:, chunk, 1:2]
            if on_vector:
                nc.vector.tensor_scalar(
                    out=line[:], in0=y_t[:], scalar1=line_scale, scalar2=shifts[:, chunk, 3:4], op0=ALU.mult, op1=ALU.add
                )
                nc.vector.tensor_scalar(
                    out=relu[:], in0=y_t[:], scalar1=relu_scale, scalar2=shifts[:, chunk, 2:3], op0=ALU.mult, op1=ALU.max
                )
            else:
                nc.scalar.activation(
                    out=line[:], in_=y_t[:], func=ACT.Identity, bias=shifts[:, chunk, 0:1], scale=line_scale
                )
                nc.scalar.activation(
                    out=relu[:], in_=y_t[:], func=ACT.Relu, bias=shifts[:, chunk, 1:2], scale=relu_scale
                )
            lines[(blk, chunk)] = line
            relus[(blk, chunk)] = relu

        def turn_back(blk, j):
            for chunk in range(CHUNKS):
                turn_chunk_back(blk, j, chunk)

        def turn_chunk_back(blk, j, chunk):
            with_x = blk in X_ON_TENSOR
            if (blk, j) not in turned_back:
                turned_back[(blk, j)] = turn_psum.tile([P, D], F32, name="back", tag="turn")
                if with_x:
                    nc.tensor.matmul(
                        out=turned_back[(blk, j)][:], lhsT=flip_ident[:], rhs=x_sb[blk][:, j, :], start=True, stop=False
                    )
            for term, first in ((lines[(blk, chunk)], True), (relus[(blk, chunk)], False)):
                nc.tensor.matmul(
                    out=turned_back[(blk, j)][:, chunk * P : (chunk + 1) * P], lhsT=term[:, j * P : (j + 1) * P],
                    rhs=ident_f32[:], is_transpose=True, start=first and not with_x,
                    stop=(not first) and (chunk == CHUNKS - 1 or not with_x),
                )

        def add_streams(blk, j):
            if j == 0:
                row_sums[blk] = small.tile([P, TILES], F32, name="row_sum")
            rest = res_sb[blk] if blk in X_ON_TENSOR else sums[blk]
            nc.vector.scalar_tensor_tensor(
                out=sums[blk][:, j, :], in0=turned_back[(blk, j)][:], scalar=flip[:], in1=rest[:, j, :],
                op0=ALU.mult, op1=ALU.add, accum_out=row_sums[blk][:, j : j + 1],
            )

        def deviation(blk):
            neg_mean = small.tile([P, TILES], F32, name="neg_mean")
            nc.scalar.mul(out=neg_mean[:], in_=row_sums[blk][:], mul=-1.0 / D)
            square_sum = small.tile([P, TILES], F32, name="square_sum")
            for j in range(TILES):
                unread = scrap.tile([P, D], BF16, name="unread")
                nc.scalar.activation(
                    out=unread[:], in_=sums[blk][:, j, :], func=ACT.Square, bias=neg_mean[:, j : j + 1], scale=1.0,
                    accum_out=square_sum[:, j : j + 1],
                )
            row_rstd = small.tile([P, TILES], F32, name="row_rstd")
            nc.scalar.activation(
                out=row_rstd[:], in_=square_sum[:], func=ACT.Abs_reciprocal_sqrt, bias=eps_ln[:], scale=1.0 / D
            )
            neg_means[blk] = neg_mean
            row_rstds[blk] = row_rstd

        def take_off_means(blk):
            for j in range(NORM_ON_GPSIMD[blk], TILES):
                nc.vector.scalar_tensor_tensor(
                    out=sums[blk][:, j, :], in0=sums[blk][:, j, :], scalar=neg_means[blk][:, j : j + 1], in1=ln_gain,
                    op0=ALU.add, op1=ALU.mult,
                )

        def store(blk, j):
            nc.sync.dma_start(out=by_partition(out[:, blk, :])[:, j : j + 1, :], in_=sums[blk][:, j : j + 1, :])

        def scale_and_store(blk):
            for j in range(NORM_ON_GPSIMD[blk], TILES):
                nc.vector.scalar_tensor_tensor(
                    out=sums[blk][:, j, :], in0=sums[blk][:, j, :], scalar=row_rstds[blk][:, j : j + 1], in1=ln_bias,
                    op0=ALU.mult, op1=ALU.add,
                )
                store(blk, j)

        def normalise_on_gpsimd(blk):
            for j in range(NORM_ON_GPSIMD[blk]):
                row_tile = sums[blk][:, j, :]
                rstd = row_rstds[blk][:, j : j + 1]
                if blk not in N_ON_SCALAR:
                    nc.gpsimd.tensor_scalar(
                        out=row_tile, in0=row_tile, scalar1=neg_means[blk][:, j : j + 1], scalar2=rstd,
                        op0=ALU.add, op1=ALU.mult,
                    )
                    nc.gpsimd.tensor_tensor(out=row_tile, in0=row_tile, in1=ln_sb[:, 0, :], op=ALU.mult)
                    nc.gpsimd.tensor_tensor(out=row_tile, in0=row_tile, in1=ln_sb[:, 1, :], op=ALU.add)
                    continue
                offset = small.tile([P, 1], F32, name="offset%d" % j)
                nc.scalar.activation(out=offset[:], in_=neg_means[blk][:, j : j + 1], func=ACT.Copy, scale=rstd)
                nc.scalar.activation(out=row_tile, in_=row_tile, func=ACT.Identity, scale=rstd, bias=offset[:])
                nc.gpsimd.tensor_tensor(out=row_tile, in0=row_tile, in1=ln_sb[:, 0, :], op=ALU.mult)
                nc.gpsimd.tensor_tensor(out=row_tile, in0=row_tile, in1=ln_sb[:, 1, :], op=ALU.add)

        first_late, second_late = LATE

        def late_statistics(blk, chunk):
            take_statistics(blk, chunk, conv_pass(blk, chunk, turn_psum, "turn"))

        def turn_block_0(chunk):
            for j in range(TILES):
                turn_chunk_back(0, j, chunk)

        late_statistics(first_late, 0)
        late_statistics(second_late, 0)
        late_statistics(first_late, 1)
        aggregate(0)
        late_statistics(second_late, 1)
        make_scales(0)
        late_statistics(first_late, 2)
        make_shifts(0)
        aggregate(1)
        affine(0, 0)
        late_statistics(second_late, 2)
        make_scales(1)
        late_statistics(first_late, LAST)
        make_shifts(1)
        aggregate(2)
        affine(0, 1)
        late_statistics(second_late, LAST)
        make_scales(2)
        turn_block_0(0)
        make_shifts(2)
        aggregate(LAST)
        affine(0, 2, on_vector=True)
        affine(1, 0)
        turn_block_0(1)
        make_scales(LAST)
        make_shifts(LAST)
        affine(0, LAST, on_vector=True)
        turn_block_0(2)
        affine(1, LAST, on_vector=True)
        affine(1, 1)
        turn_block_0(LAST)
        affine(1, 2)
        for j in range(TILES):
            add_streams(0, j)
        deviation(0)
        affine(2, LAST, on_vector=True)
        affine(2, 2, on_vector=True)
        for j in range(TILES):
            turn_back(1, j)
        affine(2, 0)
        affine(2, 1)
        for j in range(TILES):
            add_streams(1, j)

        for step in range(BLOCKS):
            nxt = step + 3
            shared = nxt in ON_VECTOR
            if 0 < step:
                if step + 1 < BLOCKS:
                    for j in range(TILES):
                        add_streams(step + 1, j)
                deviation(step)
            normalise_on_gpsimd(step)
            if shared:
                affine(nxt, LAST, on_vector=True)
            take_off_means(step)
            scale_and_store(step)
            for j in range(NORM_ON_GPSIMD[step]):
                store(step, j)
            for pair in ((0, 1), (2, LAST)):
                if nxt < BLOCKS:
                    for chunk in pair:
                        if (nxt, chunk) not in lines:
                            affine(nxt, chunk)
                if step + 2 < BLOCKS:
                    for j in pair:
                        turn_back(step + 2, j)
